import numpy as np
import ml_dtypes


def mxq(x, axis, fmt="e4m3"):
    dtype, down = {"e4m3": (ml_dtypes.float8_e4m3fn, 7), "e5m2": (ml_dtypes.float8_e5m2, 14)}[fmt]
    v = np.moveaxis(np.asarray(x, np.float32).astype(ml_dtypes.bfloat16).astype(np.float64), axis, -1)
    blocks = v.reshape(v.shape[:-1] + (-1, 32))
    amax = np.abs(blocks).max(-1, keepdims=True)
    byte = np.maximum(np.where(amax > 0, np.frexp(amax)[1] - 1 + 127, 0) - down, 1)
    scale = np.exp2(byte - 127.0)
    codes = (blocks / scale).astype(np.float32).astype(dtype).astype(np.float64)
    return np.moveaxis((codes * scale).reshape(v.shape), -1, axis)


WIDE = False


def mx_kscale(k):
    if not WIDE:
        return np.ones(k)
    levels = np.array([10, -10, 5, -5, 0])
    if k % 512:
        return np.exp2(np.random.permutation(np.resize(levels, k // 32))).repeat(32)
    a = np.empty((k // 512, 16))
    for p in range(k // 512):
        a[p, :8] = np.random.permutation(np.resize(levels, 8))
        for g in range(8):
            far = levels[np.abs(levels - a[p, g]) >= 10]
            a[p, g + 8] = far[np.random.randint(len(far))]
    return np.exp2(a.ravel()).repeat(32)


BF16 = ml_dtypes.bfloat16


def bf(x):
    return np.asarray(x, np.float32).astype(BF16)


def f64(x):
    return np.asarray(x).astype(np.float64)


E2M1 = np.array([0.0, 0.5, 1.0, 1.5, 2.0, 3.0, 4.0, 6.0, -0.0, -0.5, -1.0, -1.5, -2.0, -3.0, -4.0, -6.0])


def pack_weight(w, fmt):
    k, n = w.shape
    w = f64(bf(w)).reshape(k // 32, 32, n)
    amax = np.abs(w).max(1)
    if fmt == "e4m3":
        byte = np.frexp(amax)[1] - 1 + 127 - 7
    else:
        mant, ex = np.frexp(amax / 6.0)
        byte = np.where(mant > 0.5, ex, ex - 1) + 127
    byte = np.clip(np.where(amax > 0, byte, 1), 1, 254)
    scaled = (w * np.exp2(127.0 - byte)[:, None, :]).reshape(k, n).astype(np.float32)
    by_word = np.ascontiguousarray(scaled.reshape(k // 512, 128, 4, n).transpose(0, 1, 3, 2))
    if fmt == "e4m3":
        words = by_word.astype(ml_dtypes.float8_e4m3fn).view(np.uint8)
    else:
        c = by_word.astype(ml_dtypes.float4_e2m1fn).view(np.uint8) & 0xF
        words = c[..., 0::2] | (c[..., 1::2] << 4)
    return np.ascontiguousarray(words), np.ascontiguousarray(byte.astype(np.uint8).reshape(k // 512, 16, n))


def unpack_weight(words, scales, fmt):
    g, p, n, _ = words.shape
    if fmt == "e4m3":
        vals = np.ascontiguousarray(words).view(ml_dtypes.float8_e4m3fn).astype(np.float64)
    else:
        nib = np.empty((g, p, n, 4), np.uint8)
        nib[..., 0::2] = words & 0xF
        nib[..., 1::2] = words >> 4
        vals = E2M1[nib]
    vals = vals * np.repeat(np.exp2(scales.astype(np.float64) - 127.0), 8, axis=1)[..., None]
    return vals.transpose(0, 1, 3, 2).reshape(g * 512, n)
def pack4(w):
    words, scales = pack_weight(w, "e2m1")
    return words.reshape(words.shape[0], 128, -1), scales


def unpack4(words, scales):
    return unpack_weight(words.reshape(words.shape[0], 128, -1, 2), scales, "e2m1")


B, S, H, HD, LAT = 2, 2048, 4, 128, 512
HID = H * HD
ROT = HD // 2
HALF = ROT // 2
BASE = 10000.0


def make_rotary():
    inv_freq = 1.0 / BASE ** (np.arange(0, ROT, 2) / ROT)
    ang = np.arange(S)[:, None] * inv_freq[None, :]
    return np.concatenate([np.sin(ang), np.cos(ang)], axis=-1)[None, None, :, :]


def apply_rope(x, emb):
    x1, x2 = x[..., :HALF], x[..., HALF:]
    sin = emb[..., :HALF].transpose(0, 2, 1, 3)
    cos = emb[..., HALF:].transpose(0, 2, 1, 3)
    return np.concatenate([x1 * cos - x2 * sin, x1 * sin + x2 * cos], axis=-1)


def draw0():
    s, t = mx_kscale(HID), mx_kscale(LAT)
    hidden_states = bf(np.random.standard_normal((B, S, HID)) * s)
    rotary_emb = bf(make_rotary())
    W_kv_d_words, W_kv_d_scales = pack4(np.random.standard_normal((HID, LAT)) / np.sqrt(HID) / s[:, None] * t)
    W_k_u_words, W_k_u_scales = pack4(np.random.standard_normal((LAT, H * ROT)) / np.sqrt(LAT) / t[:, None])
    W_v_u_words, W_v_u_scales = pack4(np.random.standard_normal((LAT, H * HD)) / np.sqrt(LAT) / t[:, None])
    W_rope_k_words, W_rope_k_scales = pack4(np.random.standard_normal((HID, H * ROT)) / np.sqrt(HID) / s[:, None])
    return {"hidden_states": hidden_states,
            "rotary_emb": rotary_emb,
            "W_kv_d_words": W_kv_d_words,
            "W_kv_d_scales": W_kv_d_scales,
            "W_k_u_words": W_k_u_words,
            "W_k_u_scales": W_k_u_scales,
            "W_v_u_words": W_v_u_words,
            "W_v_u_scales": W_v_u_scales,
            "W_rope_k_words": W_rope_k_words,
            "W_rope_k_scales": W_rope_k_scales}


def core(hidden_states, rotary_emb, W_kv_d_words, W_kv_d_scales, W_k_u_words, W_k_u_scales, W_v_u_words, W_v_u_scales, W_rope_k_words, W_rope_k_scales):
    emb = f64(rotary_emb)
    xq = mxq(f64(hidden_states), 2, "e4m3")
    kv_d = xq @ unpack4(W_kv_d_words, W_kv_d_scales)
    kvq = mxq(kv_d, 2, "e4m3")
    k_c = (kvq @ unpack4(W_k_u_words, W_k_u_scales)).reshape(B, S, H, ROT)
    v = (kvq @ unpack4(W_v_u_words, W_v_u_scales)).reshape(B, S, H, HD)
    k_r = (xq @ unpack4(W_rope_k_words, W_rope_k_scales)).reshape(B, S, H, ROT)
    k_r = apply_rope(k_r, emb)
    k = np.concatenate([k_c, k_r], axis=-1)
    return k, v


def e4m3fn_bytes(y):
    return np.clip(np.asarray(y, np.float64), -448.0, 448.0).astype(np.float32).astype(ml_dtypes.float8_e4m3fn).view(np.uint8)


def e4m3fn_values(b):
    return np.asarray(b, np.uint8).view(ml_dtypes.float8_e4m3fn).astype(np.float64)


def setup_inputs():
    d = draw0()
    x0 = np.asarray(d['hidden_states']).astype(np.float64)
    s = (np.max(np.abs(x0), axis=(0, 1), keepdims=True) / 448.0).astype(np.float32)
    out = {}
    for k, v in d.items():
        if k == 'hidden_states':
            out['hidden_states_bytes'] = e4m3fn_bytes(x0 / s.astype(np.float64))
            out['hidden_states_scale'] = s
        else:
            out[k] = v
    return out


def reference(hidden_states_bytes, hidden_states_scale, rotary_emb, W_kv_d_words, W_kv_d_scales, W_k_u_words, W_k_u_scales, W_v_u_words, W_v_u_scales, W_rope_k_words, W_rope_k_scales):
    return core(e4m3fn_values(hidden_states_bytes) * hidden_states_scale.astype(np.float64), rotary_emb, W_kv_d_words, W_kv_d_scales, W_k_u_words, W_k_u_scales, W_v_u_words, W_v_u_scales, W_rope_k_words, W_rope_k_scales)

@@ -1,0 +1,317 @@
+from contextlib import ExitStack
+
+import concourse.mybir as mybir
+from concourse.masks import make_identity
+
+F32 = mybir.dt.float32
+BF16 = mybir.dt.bfloat16
+I32 = mybir.dt.int32
+U32 = mybir.dt.uint32
+U8 = mybir.dt.uint8
+FP8 = mybir.dt.float8_e4m3fn
+FP8X4 = mybir.dt.float8_e4m3fn_x4
+FP4X4 = mybir.dt.float4_e2m1fn_x4
+ADD = mybir.AluOpType.add
+SUB = mybir.AluOpType.subtract
+MULT = mybir.AluOpType.mult
+
+B, S, H, HD, HID, LAT = 2, 2048, 4, 128, 512, 512
+ROT, HALF = 64, 32
+P = 128
+R = S // P
+FLOPS = 2 * B * S * HID * (LAT + H * ROT + H * HD + H * ROT)
+
+PAIR = 2
+NP = B * R // PAIR
+SCALAR_WIDENS = (1, 2, 3, 4, 5, 7, 10)
+VECTOR_COPIES = {("kc", 14, 1), ("v", 13, 1), ("v", 14, 1), ("v", 15, 0), ("k", 15, 0)}
+
+
+def tile_llamaattention_pb_t_w4_kernel(
+    tc, x_bytes, x_scale, emb, wkv_words, wkv_scales, wk_words, wk_scales,
+    wv_words, wv_scales, wr_words, wr_scales, k_out, v_out,
+):
+    nc = tc.nc
+    with ExitStack() as ctx:
+        keep = ctx.enter_context(tc.tile_pool(name="keep", bufs=1))
+        work = ctx.enter_context(tc.tile_pool(name="work", bufs=3))
+        psum = ctx.enter_context(tc.psum_pool(name="psum", bufs=1))
+        ctx.enter_context(tc.manual_schedule())
+
+
+        planes = keep.tile([P, 1536], U8, align_bytes=64)
+        nc.vector.memset(planes[:].bitcast(I32), 0)
+        PL = {"kv": (0, 512), "v": (512, 1024), "k": (1024, 1280), "r": (1280, 1536)}
+
+        xb = [keep.tile([P, R, HID], U8, name="xb%d" % b) for b in range(B)]
+        x_view = [x_bytes[b].rearrange("(p r) k -> p r k", p=P) for b in range(B)]
+        xsc = keep.tile([P, 4], F32)
+        w_kv_raw = keep.tile([P, 1024], U8, align_bytes=64)
+        w_kv = keep.tile([P, 1024], U8, align_bytes=64)
+        s_kv = keep.tile([P, 512], U8, align_bytes=64)
+        w_v = keep.tile([P, 1024], U8, align_bytes=64)
+        w_k = keep.tile([P, 512], U8, align_bytes=64)
+        w_r_raw = keep.tile([P, 512], U8, align_bytes=64)
+        w_r = keep.tile([P, 512], U8, align_bytes=64)
+        s_r = keep.tile([P, 256], U8, align_bytes=64)
+        embt = keep.tile([P, R, 2, HALF], BF16)
+        tab = keep.tile([P, R, 3, HALF], F32)
+
+        nc.gpsimd.dma_start(out=xsc[:], in_=x_scale.rearrange("a b (p t) -> p (a b t)", t=4))
+        ident = keep.tile([P, P], F32)
+        make_identity(nc, ident[:])
+        nc.gpsimd.dma_start(
+            out=embt[:].rearrange("p r w j -> p r (w j)"),
+            in_=emb[0, 0].rearrange("(p r) c -> p r c", p=P),
+        )
+
+        def load_x(b, r0, r1):
+            nc.sync.dma_start(out=xb[b][:, r0:r1, :], in_=x_view[b][:, r0:r1, :])
+
+        def load_words(tile, src):
+            nc.sync.dma_start(out=tile[:].bitcast(I32), in_=src[0].bitcast(I32))
+
+        def load_scales(which, src):
+            lo, hi = PL[which]
+            for q in range(4):
+                nc.sync.dma_start(
+                    out=planes[32 * q : 32 * q + 4, lo:hi].bitcast(I32),
+                    in_=src[0, 4 * q : 4 * q + 4, :].bitcast(I32),
+                )
+
+        load_x(0, 0, 2)
+        load_words(w_kv_raw, wkv_words)
+        load_scales("kv", wkv_scales)
+        load_x(0, 2, 4)
+        load_x(0, 4, 8)
+        load_words(w_v, wv_words)
+        load_scales("v", wv_scales)
+        load_words(w_r_raw, wr_words)
+        load_x(0, 8, 16)
+        load_scales("r", wr_scales)
+        load_words(w_k, wk_words)
+        load_scales("k", wk_scales)
+        load_x(1, 0, 8)
+        load_x(1, 8, 16)
+
+        sin, cos = embt[:, :, 0, :], embt[:, :, 1, :]
+        nc.gpsimd.tensor_tensor(out=tab[:, :, 1, :], in0=sin, in1=cos, op=SUB)
+        nc.gpsimd.tensor_tensor(out=tab[:, :, 2, :], in0=sin, in1=cos, op=ADD)
+
+        xw, xT, xs, xq, kvp, kvb, kvq, krp, kt, vt, outp, m = {}, {}, {}, {}, {}, {}, {}, {}, {}, {}, {}, {}
+
+        def where(n):
+            return n // (R // PAIR), PAIR * (n % (R // PAIR))
+
+        def copy_out(which, out, in_):
+            if which in VECTOR_COPIES:
+                nc.vector.tensor_copy(out=out, in_=in_)
+            else:
+                nc.scalar.copy(out=out, in_=in_)
+
+        def widen(n):
+            b, r = where(n)
+            xw[n] = work.tile([P, PAIR * HID], BF16, name="xw", bufs=5)
+            src = xb[b][:, r : r + PAIR, :].bitcast(FP8).rearrange("p l k -> p (l k)")
+            if n in SCALAR_WIDENS:
+                nc.scalar.copy(out=xw[n][:], in_=src)
+            else:
+                nc.vector.tensor_copy(out=xw[n][:], in_=src)
+
+        def transposes(n):
+            if n in (1, 2):
+                xT[n] = psum.tile([P, 2, PAIR, P], F32, name="xTv", tag="vp", bufs=2)
+            else:
+                xT[n] = psum.tile([P, 2, PAIR, P], F32, name="xT", tag="xT", bufs=1)
+            words = xw[n][:].bitcast(F32)
+            for l in range(PAIR):
+                for u in range(2):
+                    cols = words[:, 256 * l + u : 256 * (l + 1) : 2]
+                    nc.tensor.transpose(xT[n][:, u, l, :], cols, ident[:])
+
+        def xscale(n):
+            xs[n] = work.tile([P, PAIR * P, 2, 2], BF16, name="xs", bufs=2, align_bytes=64)
+            nc.vector.tensor_tensor(
+                out=xs[n][:],
+                in0=xT[n][:].bitcast(BF16).rearrange("p u l (n e) -> p (l n) u e", e=2),
+                in1=xsc[:].rearrange("p (u e) -> p u e", u=2).unsqueeze(1).broadcast_to([P, PAIR * P, 2, 2]),
+                op=MULT,
+            )
+
+        def quantx(n):
+            codes = work.tile([P, PAIR * P], U32, name="xcodes", bufs=5, align_bytes=64)
+            scales = work.tile([P, PAIR * P], U8, name="xscales", bufs=5, align_bytes=64)
+            xq[n] = (codes, scales)
+            nc.vector.quantize_mx(
+                out=codes[:].bitcast(FP8X4), scales=scales[:],
+                in_=xs[n][:].rearrange("p n u e -> p (n u e)"),
+            )
+
+        def kv_matmuls(n):
+            codes, scales = xq[n]
+            kvp[n] = []
+            for l in range(PAIR):
+                cols = slice(l * P, (l + 1) * P)
+                bank = psum.tile([P, 4, P], F32, name="kvp", bufs=2)
+                kvp[n].append(bank)
+                for t in range(4):
+                    nc.tensor.matmul_mx(
+                        bank[:, t, :],
+                        lhsT=w_kv[:, 256 * t : 256 * (t + 1)].bitcast(FP4X4),
+                        lhsT_scale=s_kv[:, P * t : P * (t + 1)],
+                        rhs=codes[:, cols].bitcast(FP8X4),
+                        rhs_scale=scales[:, cols],
+                        start=True, stop=True,
+                    )
+
+        def kv_copy(n, l):
+            if l == 0:
+                kvb[n] = work.tile([P, PAIR * P, 4], BF16, name="kvb", bufs=2, align_bytes=64)
+            copy_out(
+                ("kc", n, l),
+                kvb[n][:, l * P : (l + 1) * P, :],
+                kvp[n][l][:].rearrange("p t n -> p n t"),
+            )
+
+        def quantkv(n):
+            codes = work.tile([P, PAIR * P], U32, name="kcodes", bufs=2, align_bytes=64)
+            scales = work.tile([P, PAIR * P], U8, name="kscales", bufs=2, align_bytes=64)
+            kvq[n] = (codes, scales)
+            nc.vector.quantize_mx(
+                out=codes[:].bitcast(FP8X4), scales=scales[:],
+                in_=kvb[n][:].rearrange("p n t -> p (n t)"),
+            )
+
+        def token_matmul(out, q, l, words, which):
+            codes, scales = q
+            cols = slice(l * P, (l + 1) * P)
+            lo, hi = PL[which]
+            nc.tensor.matmul_mx(
+                out,
+                lhsT=codes[:, cols].bitcast(FP8X4), lhsT_scale=scales[:, cols],
+                rhs=words[:].bitcast(FP4X4), rhs_scale=planes[:, lo:hi],
+                start=True, stop=True,
+            )
+
+        def kr_matmuls(n):
+            krp[n] = []
+            codes, scales = xq[n]
+            for l in range(PAIR):
+                bank = psum.tile([P, 3, H, HALF], F32, name="krp", bufs=2)
+                krp[n].append(bank)
+                cols = slice(l * P, (l + 1) * P)
+                for out, lo, hi, start, stop in (
+                    (bank[:, 1:3].rearrange("p c h j -> p (c h j)"), 0, 256, True, True),
+                    (bank[:, 0].rearrange("p h j -> p (h j)"), 0, 128, True, False),
+                    (bank[:, 0].rearrange("p h j -> p (h j)"), 128, 256, False, True),
+                ):
+                    nc.tensor.matmul_mx(
+                        out,
+                        lhsT=codes[:, cols].bitcast(FP8X4), lhsT_scale=scales[:, cols],
+                        rhs=w_r[:, 2 * lo : 2 * hi].bitcast(FP4X4), rhs_scale=s_r[:, lo:hi],
+                        start=start, stop=stop,
+                    )
+
+        def rope_product(n, l):
+            b, r = where(n)
+            if l == 0:
+                m[n] = work.tile([P, PAIR, 3, H, HALF], F32, name="m", bufs=3)
+            nc.vector.tensor_tensor(
+                out=m[n][:, l], in0=krp[n][l][:],
+                in1=tab[:, r + l].unsqueeze(2).broadcast_to([P, 3, H, HALF]),
+                op=MULT,
+            )
+
+        def rope_sums(n):
+            kt[n] = work.tile([P, PAIR, H, HD], F32, name="kt", bufs=4)
+            ko, mv = kt[n][:], m[n][:]
+            nc.gpsimd.tensor_tensor(
+                out=ko[:, :, :, ROT : ROT + HALF], in0=mv[:, :, 0], in1=mv[:, :, 2], op=SUB)
+            nc.gpsimd.tensor_tensor(
+                out=ko[:, :, :, ROT + HALF :], in0=mv[:, :, 0], in1=mv[:, :, 1], op=ADD)
+
+        def out_matmuls(n):
+            vt[n] = work.tile([P, PAIR, H * HD], F32, name="vt", bufs=4)
+            outp[n] = []
+            for l in range(PAIR):
+                bank = psum.tile([P, 512], F32, name="vp", tag="vp", bufs=2)
+                outp[n].append(bank)
+                token_matmul(bank[:], kvq[n], l, w_v, "v")
+            bank = psum.tile([P, PAIR, H, ROT], F32, name="kcp", bufs=1)
+            outp[n].append(bank)
+            for l in range(PAIR):
+                token_matmul(bank[:, l].rearrange("p h d -> p (h d)"), kvq[n], l, w_k, "k")
+
+        def out_copies(n):
+            for l in range(PAIR):
+                copy_out(("v", n, l), vt[n][:, l, :], outp[n][l][:])
+            copy_out(
+                ("k", n, 0),
+                kt[n][:].rearrange("p l h d -> p (l h) d")[:, :, 0:ROT],
+                outp[n][2][:].rearrange("p l h d -> p (l h) d"),
+            )
+
+        def store(n):
+            b, r = where(n)
+            vo = v_out[b].rearrange("(p r) h d -> p r (h d)", p=P)
+            ko = k_out[b].rearrange("(p r) h d -> p r (h d)", p=P)
+            for l0, l1 in ((0, 1), (1, 2)) if n == NP - 1 else ((0, PAIR),):
+                nc.sync.dma_start(out=vo[:, r + l0 : r + l1, :], in_=vt[n][:, l0:l1])
+            for l0, l1 in ((0, 1), (1, 2)) if n == NP - 1 else ((0, PAIR),):
+                nc.sync.dma_start(
+                    out=ko[:, r + l0 : r + l1, :],
+                    in_=kt[n][:, l0:l1].rearrange("p l h d -> p l (h d)"))
+
+        def have(n):
+            return 0 <= n < NP
+
+        for i in range(-4, NP + 1):
+            if i == -3:
+                nc.vector.tensor_copy(
+                    out=w_kv[:].rearrange("p (t m c) -> p t m c", t=4, c=2),
+                    in_=w_kv_raw[:].rearrange("p (m t c) -> p t m c", t=4, c=2))
+                nc.vector.tensor_copy(
+                    out=s_kv[:].rearrange("p (t m) -> p t m", t=4),
+                    in_=planes[:, 0:512].rearrange("p (m t) -> p t m", t=4))
+            if have(i):
+                kv_copy(i, 0)
+            if have(i + 2):
+                xscale(i + 2)
+            if have(i):
+                kv_copy(i, 1)
+            if have(i - 1):
+                out_matmuls(i - 1)
+            if have(i - 1) and i < NP:
+                rope_product(i - 1, 0)
+            if have(i + 4):
+                widen(i + 4)
+            if i == -1:
+                nc.scalar.copy(out=tab[:, :, 0, :], in_=cos)
+            if have(i + 2):
+                quantx(i + 2)
+            if have(i + 3):
+                transposes(i + 3)
+            if have(i - 1) and i < NP:
+                rope_product(i - 1, 1)
+                rope_sums(i - 1)
+            if have(i):
+                quantkv(i)
+            if have(i + 1):
+                kv_matmuls(i + 1)
+            if have(i - 1):
+                out_copies(i - 1)
+            if i == 0:
+                nc.vector.tensor_copy(
+                    out=w_r[:].bitcast(I32).rearrange("p (a h c) -> p a h c", a=2, h=H),
+                    in_=w_r_raw[:].bitcast(I32).rearrange("p (h a c) -> p a h c", a=2, h=H))
+                nc.vector.tensor_copy(
+                    out=s_r[:].bitcast(I32).rearrange("p (a h c) -> p a h c", a=2, h=H),
+                    in_=planes[:, 1280:1536].bitcast(I32).rearrange("p (h a c) -> p a h c", a=2, h=H))
+            if have(i):
+                kr_matmuls(i)
+            if i == NP - 1:
+                rope_product(i, 0)
+                rope_product(i, 1)
+                rope_sums(i)
+            if have(i - 1):
+                store(i - 1)

@@ -22,9 +22,9 @@ R = S // P
 FLOPS = 2 * B * S * HID * (LAT + H * ROT + H * HD + H * ROT)
 
 PAIR = 2
+TOK = PAIR * P
 NP = B * R // PAIR
-SCALAR_WIDENS = (1, 2, 3, 4, 5, 7, 10)
-VECTOR_COPIES = {("kc", 14, 1), ("v", 13, 1), ("v", 14, 1), ("v", 15, 0), ("k", 15, 0)}
+HEAD_WIDENS = 7
 
 
 def tile_llamaattention_pb_t_w4_kernel(
@@ -38,85 +38,91 @@ def tile_llamaattention_pb_t_w4_kernel(
         psum = ctx.enter_context(tc.psum_pool(name="psum", bufs=1))
         ctx.enter_context(tc.manual_schedule())
 
+        s_kv_raw = keep.tile([P, 512], U8, name="s_kv_raw", align_bytes=64)
+        s_r_raw = keep.tile([P, 256], U8, name="s_r_raw", align_bytes=64)
+        s_v = keep.tile([P, 512], U8, name="s_v", align_bytes=64)
+        s_k = keep.tile([P, 256], U8, name="s_k", align_bytes=64)
+        for plane in (s_kv_raw, s_r_raw, s_v, s_k):
+            nc.vector.memset(plane[:].bitcast(I32), 0)
 
-        planes = keep.tile([P, 1536], U8, align_bytes=64)
-        nc.vector.memset(planes[:].bitcast(I32), 0)
-        PL = {"kv": (0, 512), "v": (512, 1024), "k": (1024, 1280), "r": (1280, 1536)}
+        x_cuts = ((0, 0, 2), (0, 2, 8), (0, 8, 16), (1, 0, 8), (1, 8, 16))
+        xb = {}
+        for b, r0, r1 in x_cuts:
+            xb[b, r0] = keep.tile([P, (r1 - r0) * HID], U8, name="xb%d_%d" % (b, r0))
+        xsc = keep.tile([P, 4], F32, name="xsc")
+        w_kv_raw = keep.tile([P, 1024], U8, name="w_kv_raw", align_bytes=64)
+        w_kv = keep.tile([P, 1024], U8, name="w_kv", align_bytes=64)
+        s_kv = keep.tile([P, 512], U8, name="s_kv", align_bytes=64)
+        w_v = keep.tile([P, 1024], U8, name="w_v", align_bytes=64)
+        w_k = keep.tile([P, 512], U8, name="w_k", align_bytes=64)
+        w_r_raw = keep.tile([P, 512], U8, name="w_r_raw", align_bytes=64)
+        w_r = keep.tile([P, 512], U8, name="w_r", align_bytes=64)
+        s_r = keep.tile([P, 256], U8, name="s_r", align_bytes=64)
+        embt = keep.tile([P, R, 2, HALF], BF16, name="embt")
+        tab = keep.tile([P, R, 3, HALF], F32, name="tab")
+        ident = keep.tile([P, P], F32, name="ident")
 
-        xb = [keep.tile([P, R, HID], U8, name="xb%d" % b) for b in range(B)]
-        x_view = [x_bytes[b].rearrange("(p r) k -> p r k", p=P) for b in range(B)]
-        xsc = keep.tile([P, 4], F32)
-        w_kv_raw = keep.tile([P, 1024], U8, align_bytes=64)
-        w_kv = keep.tile([P, 1024], U8, align_bytes=64)
-        s_kv = keep.tile([P, 512], U8, align_bytes=64)
-        w_v = keep.tile([P, 1024], U8, align_bytes=64)
-        w_k = keep.tile([P, 512], U8, align_bytes=64)
-        w_r_raw = keep.tile([P, 512], U8, align_bytes=64)
-        w_r = keep.tile([P, 512], U8, align_bytes=64)
-        s_r = keep.tile([P, 256], U8, align_bytes=64)
-        embt = keep.tile([P, R, 2, HALF], BF16)
-        tab = keep.tile([P, R, 3, HALF], F32)
+        def load_x(i):
+            b, r0, r1 = x_cuts[i]
+            rows = x_bytes[b].rearrange("(p r) k -> p r k", p=P)[:, r0:r1, :]
+            nc.sync.dma_start(out=xb[b, r0][:].rearrange("p (r k) -> p r k", k=HID), in_=rows)
 
-        nc.gpsimd.dma_start(out=xsc[:], in_=x_scale.rearrange("a b (p t) -> p (a b t)", t=4))
-        ident = keep.tile([P, P], F32)
-        make_identity(nc, ident[:])
-        nc.gpsimd.dma_start(
-            out=embt[:].rearrange("p r w j -> p r (w j)"),
-            in_=emb[0, 0].rearrange("(p r) c -> p r c", p=P),
-        )
+        def load_words(eng, tile, src):
+            eng.dma_start(out=tile[:].bitcast(I32), in_=src[0].bitcast(I32))
 
-        def load_x(b, r0, r1):
-            nc.sync.dma_start(out=xb[b][:, r0:r1, :], in_=x_view[b][:, r0:r1, :])
-
-        def load_words(tile, src):
-            nc.sync.dma_start(out=tile[:].bitcast(I32), in_=src[0].bitcast(I32))
-
-        def load_scales(which, src):
-            lo, hi = PL[which]
+        def load_scales(eng, plane, src):
             for q in range(4):
-                nc.sync.dma_start(
-                    out=planes[32 * q : 32 * q + 4, lo:hi].bitcast(I32),
+                eng.dma_start(
+                    out=plane[32 * q : 32 * q + 4, :].bitcast(I32),
                     in_=src[0, 4 * q : 4 * q + 4, :].bitcast(I32),
                 )
 
-        load_x(0, 0, 2)
-        load_words(w_kv_raw, wkv_words)
-        load_scales("kv", wkv_scales)
-        load_x(0, 2, 4)
-        load_x(0, 4, 8)
-        load_words(w_v, wv_words)
-        load_scales("v", wv_scales)
-        load_words(w_r_raw, wr_words)
-        load_x(0, 8, 16)
-        load_scales("r", wr_scales)
-        load_words(w_k, wk_words)
-        load_scales("k", wk_scales)
-        load_x(1, 0, 8)
-        load_x(1, 8, 16)
+        def load_emb(eng):
+            eng.dma_start(
+                out=embt[:].rearrange("p r w j -> p r (w j)"),
+                in_=emb[0, 0].rearrange("(p r) c -> p r c", p=P),
+            )
+
+        load_x(0)
+        load_words(nc.sync, w_kv_raw, wkv_words)
+        load_x(1)
+        load_scales(nc.sync, s_kv_raw, wkv_scales)
+        load_emb(nc.sync)
+        load_x(2)
+        load_words(nc.sync, w_r_raw, wr_words)
+        load_scales(nc.sync, s_r_raw, wr_scales)
+        load_words(nc.sync, w_v, wv_words)
+        load_words(nc.sync, w_k, wk_words)
+        load_scales(nc.sync, s_v, wv_scales)
+        load_scales(nc.sync, s_k, wk_scales)
+        load_x(3)
+        load_x(4)
+        nc.gpsimd.dma_start(out=xsc[:], in_=x_scale.rearrange("a b (p t) -> p (a b t)", t=4))
+        make_identity(nc, ident[:])
 
         sin, cos = embt[:, :, 0, :], embt[:, :, 1, :]
-        nc.gpsimd.tensor_tensor(out=tab[:, :, 1, :], in0=sin, in1=cos, op=SUB)
-        nc.gpsimd.tensor_tensor(out=tab[:, :, 2, :], in0=sin, in1=cos, op=ADD)
 
-        xw, xT, xs, xq, kvp, kvb, kvq, krp, kt, vt, outp, m = {}, {}, {}, {}, {}, {}, {}, {}, {}, {}, {}, {}
+        xw, xT, qin, quant, kvp, krp, kt, vt, outp, prod = {}, {}, {}, {}, {}, {}, {}, {}, {}, {}
 
         def where(n):
             return n // (R // PAIR), PAIR * (n % (R // PAIR))
 
-        def copy_out(which, out, in_):
-            if which in VECTOR_COPIES:
+        def have(n):
+            return 0 <= n < NP
+
+        def copy_on(on_vector, out, in_):
+            if on_vector:
                 nc.vector.tensor_copy(out=out, in_=in_)
             else:
                 nc.scalar.copy(out=out, in_=in_)
 
-        def widen(n):
+        def widen(n, l0, l1, on_vector):
             b, r = where(n)
-            xw[n] = work.tile([P, PAIR * HID], BF16, name="xw", bufs=5)
-            src = xb[b][:, r : r + PAIR, :].bitcast(FP8).rearrange("p l k -> p (l k)")
-            if n in SCALAR_WIDENS:
-                nc.scalar.copy(out=xw[n][:], in_=src)
-            else:
-                nc.vector.tensor_copy(out=xw[n][:], in_=src)
+            r0 = max(c[1] for c in x_cuts if c[0] == b and c[1] <= r)
+            if n not in xw:
+                xw[n] = work.tile([P, PAIR * HID], BF16, name="xw", bufs=8)
+            src = xb[b, r0][:, (r - r0 + l0) * HID : (r - r0 + l1) * HID].bitcast(FP8)
+            copy_on(on_vector, xw[n][:, l0 * HID : l1 * HID], src)
 
         def transposes(n):
             if n in (1, 2):
@@ -129,189 +135,248 @@ def tile_llamaattention_pb_t_w4_kernel(
                     cols = words[:, 256 * l + u : 256 * (l + 1) : 2]
                     nc.tensor.transpose(xT[n][:, u, l, :], cols, ident[:])
 
+        def q_tile(s):
+            if s not in qin:
+                qin[s] = work.tile([P, 2, TOK, 4], BF16, name="qin", bufs=3, align_bytes=64)
+            return qin[s]
+
         def xscale(n):
-            xs[n] = work.tile([P, PAIR * P, 2, 2], BF16, name="xs", bufs=2, align_bytes=64)
             nc.vector.tensor_tensor(
-                out=xs[n][:],
+                out=q_tile(n - 2)[:, 0].rearrange("p n (u e) -> p n u e", u=2),
                 in0=xT[n][:].bitcast(BF16).rearrange("p u l (n e) -> p (l n) u e", e=2),
-                in1=xsc[:].rearrange("p (u e) -> p u e", u=2).unsqueeze(1).broadcast_to([P, PAIR * P, 2, 2]),
+                in1=xsc[:].rearrange("p (u e) -> p u e", u=2).unsqueeze(1).broadcast_to([P, TOK, 2, 2]),
                 op=MULT,
             )
 
-        def quantx(n):
-            codes = work.tile([P, PAIR * P], U32, name="xcodes", bufs=5, align_bytes=64)
-            scales = work.tile([P, PAIR * P], U8, name="xscales", bufs=5, align_bytes=64)
-            xq[n] = (codes, scales)
+        def quantise(s):
+            codes = work.tile([P, 2, TOK], U32, name="codes", bufs=4, align_bytes=64)
+            scales = work.tile([P, 2, TOK], U8, name="scales", bufs=4, align_bytes=64)
+            quant[s] = (codes, scales)
+            lo = 0 if have(s + 2) else 1
+            hi = 2 if have(s) else 1
             nc.vector.quantize_mx(
-                out=codes[:].bitcast(FP8X4), scales=scales[:],
-                in_=xs[n][:].rearrange("p n u e -> p (n u e)"),
+                out=codes[:, lo:hi].rearrange("p a n -> p (a n)").bitcast(FP8X4),
+                scales=scales[:, lo:hi].rearrange("p a n -> p (a n)"),
+                in_=q_tile(s)[:, lo:hi].rearrange("p a n t -> p (a n t)"),
             )
 
-        def kv_matmuls(n):
-            codes, scales = xq[n]
-            kvp[n] = []
-            for l in range(PAIR):
-                cols = slice(l * P, (l + 1) * P)
-                bank = psum.tile([P, 4, P], F32, name="kvp", bufs=2)
-                kvp[n].append(bank)
-                for t in range(4):
-                    nc.tensor.matmul_mx(
-                        bank[:, t, :],
-                        lhsT=w_kv[:, 256 * t : 256 * (t + 1)].bitcast(FP4X4),
-                        lhsT_scale=s_kv[:, P * t : P * (t + 1)],
-                        rhs=codes[:, cols].bitcast(FP8X4),
-                        rhs_scale=scales[:, cols],
-                        start=True, stop=True,
-                    )
-
-        def kv_copy(n, l):
-            if l == 0:
-                kvb[n] = work.tile([P, PAIR * P, 4], BF16, name="kvb", bufs=2, align_bytes=64)
-            copy_out(
-                ("kc", n, l),
-                kvb[n][:, l * P : (l + 1) * P, :],
-                kvp[n][l][:].rearrange("p t n -> p n t"),
-            )
-
-        def quantkv(n):
-            codes = work.tile([P, PAIR * P], U32, name="kcodes", bufs=2, align_bytes=64)
-            scales = work.tile([P, PAIR * P], U8, name="kscales", bufs=2, align_bytes=64)
-            kvq[n] = (codes, scales)
-            nc.vector.quantize_mx(
-                out=codes[:].bitcast(FP8X4), scales=scales[:],
-                in_=kvb[n][:].rearrange("p n t -> p (n t)"),
-            )
-
-        def token_matmul(out, q, l, words, which):
-            codes, scales = q
+        def operand(s, a, l):
+            codes, scales = quant[s]
             cols = slice(l * P, (l + 1) * P)
-            lo, hi = PL[which]
-            nc.tensor.matmul_mx(
-                out,
-                lhsT=codes[:, cols].bitcast(FP8X4), lhsT_scale=scales[:, cols],
-                rhs=words[:].bitcast(FP4X4), rhs_scale=planes[:, lo:hi],
-                start=True, stop=True,
+            return codes[:, a, cols].bitcast(FP8X4), scales[:, a, cols]
+
+        def kv_matmuls(n, l):
+            codes, scales = operand(n - 2, 0, l)
+            kvp[n, l] = psum.tile([P, 4, P], F32, name="kvp", bufs=2)
+            for t in range(4):
+                nc.tensor.matmul_mx(
+                    kvp[n, l][:, t, :],
+                    lhsT=w_kv[:, 256 * t : 256 * (t + 1)].bitcast(FP4X4),
+                    lhsT_scale=s_kv[:, P * t : P * (t + 1)],
+                    rhs=codes, rhs_scale=scales,
+                    start=True, stop=True,
+                )
+
+        def kv_copy(n, l, on_vector):
+            copy_on(
+                on_vector,
+                q_tile(n)[:, 1, l * P : (l + 1) * P, :].rearrange("p (c i) t -> p c t i", i=2),
+                kvp[n, l][:].rearrange("p t (c i) -> p c t i", i=2),
             )
 
-        def kr_matmuls(n):
-            krp[n] = []
-            codes, scales = xq[n]
-            for l in range(PAIR):
-                bank = psum.tile([P, 3, H, HALF], F32, name="krp", bufs=2)
-                krp[n].append(bank)
-                cols = slice(l * P, (l + 1) * P)
-                for out, lo, hi, start, stop in (
-                    (bank[:, 1:3].rearrange("p c h j -> p (c h j)"), 0, 256, True, True),
-                    (bank[:, 0].rearrange("p h j -> p (h j)"), 0, 128, True, False),
-                    (bank[:, 0].rearrange("p h j -> p (h j)"), 128, 256, False, True),
-                ):
-                    nc.tensor.matmul_mx(
-                        out,
-                        lhsT=codes[:, cols].bitcast(FP8X4), lhsT_scale=scales[:, cols],
-                        rhs=w_r[:, 2 * lo : 2 * hi].bitcast(FP4X4), rhs_scale=s_r[:, lo:hi],
-                        start=start, stop=stop,
-                    )
+        def kr_matmuls(n, l):
+            codes, scales = operand(n - 2, 0, l)
+            krp[n, l] = psum.tile([P, 3, H * HALF], F32, name="krp", tag="krp", bufs=2)
+            for out, lo, hi, start, stop in (
+                (krp[n, l][:, 0:2].rearrange("p c m -> p (c m)"), 0, 256, True, True),
+                (krp[n, l][:, 2], 0, 128, True, False),
+                (krp[n, l][:, 2], 128, 256, False, True),
+            ):
+                nc.tensor.matmul_mx(
+                    out, lhsT=codes, lhsT_scale=scales,
+                    rhs=w_r[:, 2 * lo : 2 * hi].bitcast(FP4X4), rhs_scale=s_r[:, lo:hi],
+                    start=start, stop=stop,
+                )
 
         def rope_product(n, l):
             b, r = where(n)
             if l == 0:
-                m[n] = work.tile([P, PAIR, 3, H, HALF], F32, name="m", bufs=3)
+                prod[n] = work.tile([P, PAIR, H, 3, HALF], F32, name="prod", bufs=2)
             nc.vector.tensor_tensor(
-                out=m[n][:, l], in0=krp[n][l][:],
+                out=prod[n][:, l].rearrange("p h c j -> p c h j"),
+                in0=krp[n, l][:].rearrange("p c (h j) -> p c h j", h=H),
                 in1=tab[:, r + l].unsqueeze(2).broadcast_to([P, 3, H, HALF]),
                 op=MULT,
             )
 
         def rope_sums(n):
-            kt[n] = work.tile([P, PAIR, H, HD], F32, name="kt", bufs=4)
-            ko, mv = kt[n][:], m[n][:]
+            kt[n] = work.tile([P, PAIR, H, HD], F32, name="kt", bufs=5)
+            m = prod[n][:].rearrange("p l h c j -> p (l h) c j")
             nc.gpsimd.tensor_tensor(
-                out=ko[:, :, :, ROT : ROT + HALF], in0=mv[:, :, 0], in1=mv[:, :, 2], op=SUB)
-            nc.gpsimd.tensor_tensor(
-                out=ko[:, :, :, ROT + HALF :], in0=mv[:, :, 0], in1=mv[:, :, 1], op=ADD)
-
-        def out_matmuls(n):
-            vt[n] = work.tile([P, PAIR, H * HD], F32, name="vt", bufs=4)
-            outp[n] = []
-            for l in range(PAIR):
-                bank = psum.tile([P, 512], F32, name="vp", tag="vp", bufs=2)
-                outp[n].append(bank)
-                token_matmul(bank[:], kvq[n], l, w_v, "v")
-            bank = psum.tile([P, PAIR, H, ROT], F32, name="kcp", bufs=1)
-            outp[n].append(bank)
-            for l in range(PAIR):
-                token_matmul(bank[:, l].rearrange("p h d -> p (h d)"), kvq[n], l, w_k, "k")
-
-        def out_copies(n):
-            for l in range(PAIR):
-                copy_out(("v", n, l), vt[n][:, l, :], outp[n][l][:])
-            copy_out(
-                ("k", n, 0),
-                kt[n][:].rearrange("p l h d -> p (l h) d")[:, :, 0:ROT],
-                outp[n][2][:].rearrange("p l h d -> p (l h) d"),
+                out=kt[n][:].rearrange("p l h (a j) -> p (l h) a j", j=HALF)[:, :, 2:4, :],
+                in0=m[:, :, 2:3, :].broadcast_to([P, PAIR * H, 2, HALF]),
+                in1=m[:, :, 0:2, :],
+                op=SUB,
             )
 
-        def store(n):
+        def v_matmul(n, l, spare=False):
+            codes, scales = operand(n, 1, l)
+            if spare:
+                outp[n, l] = psum.tile([P, 512], F32, name="vx", tag="xT", bufs=1)
+            else:
+                outp[n, l] = psum.tile([P, 512], F32, name="vp", tag="vp", bufs=2)
+            nc.tensor.matmul_mx(
+                outp[n, l][:], lhsT=codes, lhsT_scale=scales,
+                rhs=w_v[:].bitcast(FP4X4), rhs_scale=s_v[:], start=True, stop=True,
+            )
+
+        def kc_matmuls(n):
+            outp[n, 2] = psum.tile([P, PAIR, H * ROT], F32, name="kcp", bufs=1)
+            for l in range(PAIR):
+                codes, scales = operand(n, 1, l)
+                nc.tensor.matmul_mx(
+                    outp[n, 2][:, l], lhsT=codes, lhsT_scale=scales,
+                    rhs=w_k[:].bitcast(FP4X4), rhs_scale=s_k[:], start=True, stop=True,
+                )
+
+        def v_copy(n, l, on_vector):
+            if l == 0:
+                vt[n] = work.tile([P, PAIR, H * HD], F32, name="vt", bufs=4)
+            copy_on(on_vector, vt[n][:, l, :], outp[n, l][:])
+
+        def kc_copy(n, on_vector, l0=0, l1=PAIR):
+            copy_on(
+                on_vector,
+                kt[n][:, l0:l1].rearrange("p l h d -> p (l h) d")[:, :, 0:ROT],
+                outp[n, 2][:, l0:l1].rearrange("p l (h d) -> p (l h) d", h=H),
+            )
+
+        def store_v(n, l0=0, l1=PAIR):
+            store(v_out, vt[n], n, l0, l1)
+
+        def store_k(n, l0=0, l1=PAIR):
+            store(k_out, kt[n][:].rearrange("p l h d -> p l (h d)"), n, l0, l1)
+
+        def store(out, tile, n, l0, l1):
             b, r = where(n)
-            vo = v_out[b].rearrange("(p r) h d -> p r (h d)", p=P)
-            ko = k_out[b].rearrange("(p r) h d -> p r (h d)", p=P)
-            for l0, l1 in ((0, 1), (1, 2)) if n == NP - 1 else ((0, PAIR),):
-                nc.sync.dma_start(out=vo[:, r + l0 : r + l1, :], in_=vt[n][:, l0:l1])
-            for l0, l1 in ((0, 1), (1, 2)) if n == NP - 1 else ((0, PAIR),):
-                nc.sync.dma_start(
-                    out=ko[:, r + l0 : r + l1, :],
-                    in_=kt[n][:, l0:l1].rearrange("p l h d -> p l (h d)"))
+            rows = out[b].rearrange("(p r) h d -> p r (h d)", p=P)
+            nc.sync.dma_start(out=rows[:, r + l0 : r + l1, :], in_=tile[:, l0:l1])
 
-        def have(n):
-            return 0 <= n < NP
+        def permute_kv():
+            nc.vector.tensor_copy(
+                out=w_kv[:].rearrange("p (t m c) -> p t m c", t=4, c=2),
+                in_=w_kv_raw[:].rearrange("p (m t c) -> p t m c", t=4, c=2))
+            nc.vector.tensor_copy(
+                out=s_kv[:].rearrange("p (t m) -> p t m", t=4),
+                in_=s_kv_raw[:].rearrange("p (m t) -> p t m", t=4))
 
-        for i in range(-4, NP + 1):
-            if i == -3:
-                nc.vector.tensor_copy(
-                    out=w_kv[:].rearrange("p (t m c) -> p t m c", t=4, c=2),
-                    in_=w_kv_raw[:].rearrange("p (m t c) -> p t m c", t=4, c=2))
-                nc.vector.tensor_copy(
-                    out=s_kv[:].rearrange("p (t m) -> p t m", t=4),
-                    in_=planes[:, 0:512].rearrange("p (m t) -> p t m", t=4))
-            if have(i):
-                kv_copy(i, 0)
-            if have(i + 2):
-                xscale(i + 2)
-            if have(i):
-                kv_copy(i, 1)
-            if have(i - 1):
-                out_matmuls(i - 1)
-            if have(i - 1) and i < NP:
-                rope_product(i - 1, 0)
-            if have(i + 4):
-                widen(i + 4)
-            if i == -1:
-                nc.scalar.copy(out=tab[:, :, 0, :], in_=cos)
-            if have(i + 2):
-                quantx(i + 2)
-            if have(i + 3):
-                transposes(i + 3)
-            if have(i - 1) and i < NP:
-                rope_product(i - 1, 1)
-                rope_sums(i - 1)
-            if have(i):
-                quantkv(i)
-            if have(i + 1):
-                kv_matmuls(i + 1)
-            if have(i - 1):
-                out_copies(i - 1)
-            if i == 0:
-                nc.vector.tensor_copy(
-                    out=w_r[:].bitcast(I32).rearrange("p (a h c) -> p a h c", a=2, h=H),
-                    in_=w_r_raw[:].bitcast(I32).rearrange("p (h a c) -> p a h c", a=2, h=H))
-                nc.vector.tensor_copy(
-                    out=s_r[:].bitcast(I32).rearrange("p (a h c) -> p a h c", a=2, h=H),
-                    in_=planes[:, 1280:1536].bitcast(I32).rearrange("p (h a c) -> p a h c", a=2, h=H))
-            if have(i):
-                kr_matmuls(i)
-            if i == NP - 1:
-                rope_product(i, 0)
-                rope_product(i, 1)
-                rope_sums(i)
-            if have(i - 1):
-                store(i - 1)
+        def permute_r():
+            for dst, src in ((w_r, w_r_raw), (s_r, s_r_raw)):
+                for a in range(2):
+                    nc.vector.tensor_copy(
+                        out=dst[:].bitcast(I32).rearrange("p (a h c) -> p a h c", a=2, h=H)[:, 1 - a],
+                        in_=src[:].bitcast(I32).rearrange("p (h a c) -> p a h c", a=2, h=H)[:, a])
+
+        widen(0, 0, 1, True)
+        widen(0, 1, 2, False)
+        transposes(0)
+        permute_kv()
+        nc.gpsimd.tensor_tensor(out=tab[:, :, 0, :], in0=cos, in1=sin, op=ADD)
+        for n in range(1, HEAD_WIDENS):
+            widen(n, 0, PAIR, False)
+            if n == 1:
+                transposes(n)
+            if n == 3:
+                nc.scalar.copy(out=tab[:, :, 2, :], in_=cos)
+        xscale(0)
+        quantise(-2)
+        late = [(n, l) for n in range(HEAD_WIDENS, NP) for l in range(PAIR)]
+
+        def widen_next(on_vector):
+            if late:
+                n, l = late[0]
+                late.remove(late[0])
+                widen(n, l, l + 1, on_vector)
+
+        for s in range(-1, NP - 2):
+            last = s == NP - 3
+            if have(s - 1):
+                v_matmul(s - 1, 0)
+                v_matmul(s - 1, 1)
+                kc_matmuls(s - 1)
+            xscale(s + 2)
+            if s < 0 and have(s + 3):
+                transposes(s + 3)
+            kv_matmuls(s + 1, 0)
+            kv_matmuls(s + 1, 1)
+            if s >= 0 and have(s + 3):
+                transposes(s + 3)
+            if have(s - 1):
+                v_copy(s - 1, 0, False)
+                if s >= 12:
+                    store_v(s - 1, 0, 1)
+                v_copy(s - 1, 1, False)
+                store_v(s - 1, 1 if s >= 12 else 0, 2)
+                kc_copy(s - 1, False)
+                store_k(s - 1)
+            if s >= 1 and s % 2 == 1:
+                widen_next(False)
+            if s == -1:
+                nc.vector.tensor_tensor(out=tab[:, :, 1, :], in0=cos, in1=sin, op=SUB)
+                permute_r()
+            if have(s):
+                rope_product(s, 0)
+                rope_product(s, 1)
+                rope_sums(s)
+            kv_copy(s + 1, 0, False)
+            if not last:
+                kv_copy(s + 1, 1, False)
+            kr_matmuls(s + 1, 0)
+            kr_matmuls(s + 1, 1)
+            if s >= 0:
+                widen_next(True)
+            quantise(s)
+        a, b, c = NP - 3, NP - 2, NP - 1
+        v_matmul(a, 0)
+        v_matmul(a, 1)
+        kc_matmuls(a)
+        kv_copy(b, 1, True)
+        rope_product(b, 0)
+        kv_matmuls(c, 0)
+        kv_matmuls(c, 1)
+        v_copy(a, 0, False)
+        store_v(a, 0, 1)
+        rope_product(b, 1)
+        rope_sums(b)
+        quantise(b)
+        v_copy(a, 1, False)
+        store_v(a, 1, 2)
+        kr_matmuls(c, 0)
+        kr_matmuls(c, 1)
+        kc_copy(a, True)
+        store_k(a)
+        kv_copy(c, 0, False)
+        kv_copy(c, 1, True)
+        v_matmul(b, 0)
+        v_matmul(b, 1)
+        kc_matmuls(b)
+        rope_product(c, 0)
+        rope_product(c, 1)
+        rope_sums(c)
+        quantise(c)
+        v_copy(b, 0, False)
+        store_v(b, 0, 1)
+        v_copy(b, 1, False)
+        store_v(b, 1, 2)
+        v_matmul(c, 0, True)
+        kc_copy(b, True)
+        store_k(b)
+        v_matmul(c, 1)
+        kc_matmuls(c)
+        v_copy(c, 0, False)
+        store_v(c, 0, 1)
+        v_copy(c, 1, True)
+        store_v(c, 1, 2)
+        kc_copy(c, False)
+        store_k(c, 0, 1)
+        store_k(c, 1, 2)

@@ -84,18 +84,18 @@ def tile_llamaattention_pb_t_w4_kernel(
             )
 
         load_x(0)
-        load_words(nc.sync, w_kv_raw, wkv_words)
         load_x(1)
+        load_words(nc.sync, w_kv_raw, wkv_words)
         load_scales(nc.sync, s_kv_raw, wkv_scales)
         load_emb(nc.sync)
         load_x(2)
         load_words(nc.sync, w_r_raw, wr_words)
         load_scales(nc.sync, s_r_raw, wr_scales)
         load_words(nc.sync, w_v, wv_words)
-        load_words(nc.sync, w_k, wk_words)
-        load_scales(nc.sync, s_v, wv_scales)
-        load_scales(nc.sync, s_k, wk_scales)
         load_x(3)
+        load_scales(nc.sync, s_v, wv_scales)
+        load_words(nc.sync, w_k, wk_words)
+        load_scales(nc.sync, s_k, wk_scales)
         load_x(4)
         nc.gpsimd.dma_start(out=xsc[:], in_=x_scale.rearrange("a b (p t) -> p (a b t)", t=4))
         make_identity(nc, ident[:])
@@ -103,6 +103,8 @@ def tile_llamaattention_pb_t_w4_kernel(
         sin, cos = embt[:, :, 0, :], embt[:, :, 1, :]
 
         xw, xT, qin, quant, kvp, krp, kt, vt, outp, prod = {}, {}, {}, {}, {}, {}, {}, {}, {}, {}
+
+        tiles = [(n, l) for n in range(1, NP) for l in range(PAIR)]
 
         def where(n):
             return n // (R // PAIR), PAIR * (n % (R // PAIR))
@@ -120,11 +122,12 @@ def tile_llamaattention_pb_t_w4_kernel(
             b, r = where(n)
             r0 = max(c[1] for c in x_cuts if c[0] == b and c[1] <= r)
             if n not in xw:
-                xw[n] = work.tile([P, PAIR * HID], BF16, name="xw", bufs=8)
+                xw[n] = work.tile([P, PAIR * HID], BF16, name="xw", bufs=12)
             src = xb[b, r0][:, (r - r0 + l0) * HID : (r - r0 + l1) * HID].bitcast(FP8)
             copy_on(on_vector, xw[n][:, l0 * HID : l1 * HID], src)
 
         def transposes(n):
+            assert (n, PAIR - 1) not in tiles
             if n in (1, 2):
                 xT[n] = psum.tile([P, 2, PAIR, P], F32, name="xTv", tag="vp", bufs=2)
             else:
@@ -219,6 +222,15 @@ def tile_llamaattention_pb_t_w4_kernel(
                 op=SUB,
             )
 
+        def kr_all(n):
+            kr_matmuls(n, 0)
+            kr_matmuls(n, 1)
+
+        def rope_all(n):
+            rope_product(n, 0)
+            rope_product(n, 1)
+            rope_sums(n)
+
         def v_matmul(n, l, spare=False):
             codes, scales = operand(n, 1, l)
             if spare:
@@ -262,10 +274,12 @@ def tile_llamaattention_pb_t_w4_kernel(
             rows = out[b].rearrange("(p r) h d -> p r (h d)", p=P)
             nc.sync.dma_start(out=rows[:, r + l0 : r + l1, :], in_=tile[:, l0:l1])
 
-        def permute_kv():
+        def permute_kv_words():
             nc.vector.tensor_copy(
                 out=w_kv[:].rearrange("p (t m c) -> p t m c", t=4, c=2),
                 in_=w_kv_raw[:].rearrange("p (m t c) -> p t m c", t=4, c=2))
+
+        def permute_kv_scales():
             nc.vector.tensor_copy(
                 out=s_kv[:].rearrange("p (t m) -> p t m", t=4),
                 in_=s_kv_raw[:].rearrange("p (m t) -> p t m", t=4))
@@ -277,26 +291,31 @@ def tile_llamaattention_pb_t_w4_kernel(
                         out=dst[:].bitcast(I32).rearrange("p (a h c) -> p a h c", a=2, h=H)[:, 1 - a],
                         in_=src[:].bitcast(I32).rearrange("p (h a c) -> p a h c", a=2, h=H)[:, a])
 
+
+        def widen_next(count, on_vector):
+            if tiles:
+                n, l = tiles[0]
+                for i in range(count):
+                    tiles.remove(tiles[0])
+                widen(n, l, l + count, on_vector)
+
         widen(0, 0, 1, True)
         widen(0, 1, 2, False)
         transposes(0)
-        permute_kv()
+        permute_kv_words()
+        permute_kv_scales()
         nc.gpsimd.tensor_tensor(out=tab[:, :, 0, :], in0=cos, in1=sin, op=ADD)
-        for n in range(1, HEAD_WIDENS):
-            widen(n, 0, PAIR, False)
-            if n == 1:
-                transposes(n)
-            if n == 3:
-                nc.scalar.copy(out=tab[:, :, 2, :], in_=cos)
+        nc.gpsimd.tensor_tensor(out=tab[:, :, 1, :], in0=cos, in1=sin, op=SUB)
+        widen_next(PAIR, False)
+        transposes(1)
+        widen_next(PAIR, False)
+        nc.scalar.copy(out=tab[:, :, 2, :], in_=cos)
+        widen_next(PAIR, False)
+        widen_next(PAIR, False)
+        widen_next(PAIR, False)
+        widen_next(PAIR, False)
         xscale(0)
         quantise(-2)
-        late = [(n, l) for n in range(HEAD_WIDENS, NP) for l in range(PAIR)]
-
-        def widen_next(on_vector):
-            if late:
-                n, l = late[0]
-                late.remove(late[0])
-                widen(n, l, l + 1, on_vector)
 
         for s in range(-1, NP - 2):
             last = s == NP - 3
@@ -305,7 +324,7 @@ def tile_llamaattention_pb_t_w4_kernel(
                 v_matmul(s - 1, 1)
                 kc_matmuls(s - 1)
             xscale(s + 2)
-            if s < 0 and have(s + 3):
+            if s < 0:
                 transposes(s + 3)
             kv_matmuls(s + 1, 0)
             kv_matmuls(s + 1, 1)
@@ -319,40 +338,36 @@ def tile_llamaattention_pb_t_w4_kernel(
                 store_v(s - 1, 1 if s >= 12 else 0, 2)
                 kc_copy(s - 1, False)
                 store_k(s - 1)
-            if s >= 1 and s % 2 == 1:
-                widen_next(False)
+
             if s == -1:
-                nc.vector.tensor_tensor(out=tab[:, :, 1, :], in0=cos, in1=sin, op=SUB)
                 permute_r()
             if have(s):
-                rope_product(s, 0)
-                rope_product(s, 1)
-                rope_sums(s)
+                rope_all(s)
             kv_copy(s + 1, 0, False)
             if not last:
                 kv_copy(s + 1, 1, False)
-            kr_matmuls(s + 1, 0)
-            kr_matmuls(s + 1, 1)
-            if s >= 0:
-                widen_next(True)
+            if s < 2:
+                widen_next(PAIR, False)
+            if s == 0:
+                widen_next(PAIR, False)
+            kr_all(s + 1)
+            if s >= 1:
+                widen_next(1, True)
             quantise(s)
         a, b, c = NP - 3, NP - 2, NP - 1
         v_matmul(a, 0)
         v_matmul(a, 1)
         kc_matmuls(a)
         kv_copy(b, 1, True)
-        rope_product(b, 0)
         kv_matmuls(c, 0)
         kv_matmuls(c, 1)
         v_copy(a, 0, False)
         store_v(a, 0, 1)
-        rope_product(b, 1)
-        rope_sums(b)
+        rope_all(b)
         quantise(b)
         v_copy(a, 1, False)
         store_v(a, 1, 2)
-        kr_matmuls(c, 0)
-        kr_matmuls(c, 1)
+        kr_all(c)
         kc_copy(a, True)
         store_k(a)
         kv_copy(c, 0, False)
@@ -360,9 +375,7 @@ def tile_llamaattention_pb_t_w4_kernel(
         v_matmul(b, 0)
         v_matmul(b, 1)
         kc_matmuls(b)
-        rope_product(c, 0)
-        rope_product(c, 1)
-        rope_sums(c)
+        rope_all(c)
         quantise(c)
         v_copy(b, 0, False)
         store_v(b, 0, 1)

@@ -45,7 +45,7 @@ def tile_llamaattention_pb_t_w4_kernel(
         for plane in (s_kv_raw, s_r_raw, s_v, s_k):
             nc.vector.memset(plane[:].bitcast(I32), 0)
 
-        x_cuts = ((0, 0, 2), (0, 2, 8), (0, 8, 16), (1, 0, 8), (1, 8, 16))
+        x_cuts = ((0, 0, 2), (0, 2, 4), (0, 4, 8), (0, 8, 16), (1, 0, 8), (1, 8, 16))
         xb = {}
         for b, r0, r1 in x_cuts:
             xb[b, r0] = keep.tile([P, (r1 - r0) * HID], U8, name="xb%d_%d" % (b, r0))
@@ -58,8 +58,12 @@ def tile_llamaattention_pb_t_w4_kernel(
         w_r_raw = keep.tile([P, 512], U8, name="w_r_raw", align_bytes=64)
         w_r = keep.tile([P, 512], U8, name="w_r", align_bytes=64)
         s_r = keep.tile([P, 256], U8, name="s_r", align_bytes=64)
-        embt = keep.tile([P, R, 2, HALF], BF16, name="embt")
+        EMB_CUT = 8
+        emb_rows = ((0, EMB_CUT), (EMB_CUT, R))
+        embt = [keep.tile([P, r1 - r0, 2, HALF], BF16, name="embt%d" % r0) for r0, r1 in emb_rows]
         tab = keep.tile([P, R, 3, HALF], F32, name="tab")
+        ones = keep.tile([P, 1], F32, name="ones")
+        nc.vector.memset(ones[:], 1.0)
         ident = keep.tile([P, P], F32, name="ident")
 
         def load_x(i):
@@ -77,34 +81,46 @@ def tile_llamaattention_pb_t_w4_kernel(
                     in_=src[0, 4 * q : 4 * q + 4, :].bitcast(I32),
                 )
 
-        def load_emb(eng):
-            eng.dma_start(
-                out=embt[:].rearrange("p r w j -> p r (w j)"),
-                in_=emb[0, 0].rearrange("(p r) c -> p r c", p=P),
+        def load_emb(i):
+            r0, r1 = emb_rows[i]
+            nc.sync.dma_start(
+                out=embt[i][:].rearrange("p r w j -> p r (w j)"),
+                in_=emb[0, 0].rearrange("(p r) c -> p r c", p=P)[:, r0:r1],
             )
 
         load_x(0)
-        load_x(1)
         load_words(nc.sync, w_kv_raw, wkv_words)
+        load_emb(0)
         load_scales(nc.sync, s_kv_raw, wkv_scales)
-        load_emb(nc.sync)
+        load_x(1)
         load_x(2)
+        load_emb(1)
+        load_x(3)
         load_words(nc.sync, w_r_raw, wr_words)
         load_scales(nc.sync, s_r_raw, wr_scales)
+        load_x(4)
         load_words(nc.sync, w_v, wv_words)
-        load_x(3)
         load_scales(nc.sync, s_v, wv_scales)
         load_words(nc.sync, w_k, wk_words)
         load_scales(nc.sync, s_k, wk_scales)
-        load_x(4)
+        load_x(5)
         nc.gpsimd.dma_start(out=xsc[:], in_=x_scale.rearrange("a b (p t) -> p (a b t)", t=4))
         make_identity(nc, ident[:])
 
-        sin, cos = embt[:, :, 0, :], embt[:, :, 1, :]
+        def table(eng, slot, r0, r1):
+            i = 0 if r0 < EMB_CUT else 1
+            rows = embt[i][:, r0 - emb_rows[i][0] : r1 - emb_rows[i][0]]
+            sin, cos = rows[:, :, 0, :], rows[:, :, 1, :]
+            if slot == 2:
+                nc.scalar.copy(out=tab[:, r0:r1, 2, :], in_=cos)
+            else:
+                eng.tensor_tensor(out=tab[:, r0:r1, slot, :], in0=cos, in1=sin, op=(ADD, SUB)[slot])
 
         xw, xT, qin, quant, kvp, krp, kt, vt, outp, prod = {}, {}, {}, {}, {}, {}, {}, {}, {}, {}
 
         tiles = [(n, l) for n in range(1, NP) for l in range(PAIR)]
+
+        sorted_words = set()
 
         def where(n):
             return n // (R // PAIR), PAIR * (n % (R // PAIR))
@@ -113,7 +129,9 @@ def tile_llamaattention_pb_t_w4_kernel(
             return 0 <= n < NP
 
         def copy_on(on_vector, out, in_):
-            if on_vector:
+            if on_vector == "gpsimd":
+                nc.gpsimd.tensor_copy(out=out, in_=in_)
+            elif on_vector:
                 nc.vector.tensor_copy(out=out, in_=in_)
             else:
                 nc.scalar.copy(out=out, in_=in_)
@@ -122,12 +140,18 @@ def tile_llamaattention_pb_t_w4_kernel(
             b, r = where(n)
             r0 = max(c[1] for c in x_cuts if c[0] == b and c[1] <= r)
             if n not in xw:
-                xw[n] = work.tile([P, PAIR * HID], BF16, name="xw", bufs=12)
+                xw[n] = work.tile([P, PAIR * HID], BF16, name="xw", bufs=16)
             src = xb[b, r0][:, (r - r0 + l0) * HID : (r - r0 + l1) * HID].bitcast(FP8)
-            copy_on(on_vector, xw[n][:, l0 * HID : l1 * HID], src)
+            if on_vector and n > 0:
+                sorted_words.add((n, l0))
+                nc.vector.tensor_scalar(
+                    out=xw[n][:, l0 * HID : l1 * HID].rearrange("p (u m e) -> p m u e", u=2, e=2),
+                    in0=src.rearrange("p (m u e) -> p m u e", u=2, e=2), scalar1=ones[:], scalar2=None, op0=MULT)
+            else:
+                copy_on(on_vector, xw[n][:, l0 * HID : l1 * HID], src)
 
         def transposes(n):
-            assert (n, PAIR - 1) not in tiles
+            assert (n, 0) not in tiles and (n, 1) not in tiles
             if n in (1, 2):
                 xT[n] = psum.tile([P, 2, PAIR, P], F32, name="xTv", tag="vp", bufs=2)
             else:
@@ -135,12 +159,15 @@ def tile_llamaattention_pb_t_w4_kernel(
             words = xw[n][:].bitcast(F32)
             for l in range(PAIR):
                 for u in range(2):
-                    cols = words[:, 256 * l + u : 256 * (l + 1) : 2]
+                    if (n, l) in sorted_words:
+                        cols = words[:, 256 * l + P * u : 256 * l + P * (u + 1)]
+                    else:
+                        cols = words[:, 256 * l + u : 256 * (l + 1) : 2]
                     nc.tensor.transpose(xT[n][:, u, l, :], cols, ident[:])
 
         def q_tile(s):
             if s not in qin:
-                qin[s] = work.tile([P, 2, TOK, 4], BF16, name="qin", bufs=3, align_bytes=64)
+                qin[s] = work.tile([P, 2, TOK, 4], BF16, name="qin", tag="slot%d" % (s % 4), bufs=1, align_bytes=64)
             return qin[s]
 
         def xscale(n):
@@ -213,7 +240,7 @@ def tile_llamaattention_pb_t_w4_kernel(
             )
 
         def rope_sums(n):
-            kt[n] = work.tile([P, PAIR, H, HD], F32, name="kt", bufs=5)
+            kt[n] = work.tile([P, PAIR, H, HD], F32, name="kt", tag="slot%d" % (n % 4), bufs=1, align_bytes=64)
             m = prod[n][:].rearrange("p l h c j -> p (l h) c j")
             nc.gpsimd.tensor_tensor(
                 out=kt[n][:].rearrange("p l h (a j) -> p (l h) a j", j=HALF)[:, :, 2:4, :],
@@ -229,7 +256,6 @@ def tile_llamaattention_pb_t_w4_kernel(
         def rope_all(n):
             rope_product(n, 0)
             rope_product(n, 1)
-            rope_sums(n)
 
         def v_matmul(n, l, spare=False):
             codes, scales = operand(n, 1, l)
@@ -292,33 +318,33 @@ def tile_llamaattention_pb_t_w4_kernel(
                         in_=src[:].bitcast(I32).rearrange("p (h a c) -> p a h c", a=2, h=H)[:, a])
 
 
-        def widen_next(count, on_vector):
-            if tiles:
-                n, l = tiles[0]
-                for i in range(count):
-                    tiles.remove(tiles[0])
-                widen(n, l, l + count, on_vector)
+        def widen_tiles(n, l0, l1, on_vector):
+            for l in range(l0, l1):
+                tiles.remove((n, l))
+            widen(n, l0, l1, on_vector)
 
         widen(0, 0, 1, True)
         widen(0, 1, 2, False)
         transposes(0)
         permute_kv_words()
+        table(nc.vector, 0, 0, EMB_CUT)
+        table(nc.vector, 1, 0, EMB_CUT)
         permute_kv_scales()
-        nc.gpsimd.tensor_tensor(out=tab[:, :, 0, :], in0=cos, in1=sin, op=ADD)
-        nc.gpsimd.tensor_tensor(out=tab[:, :, 1, :], in0=cos, in1=sin, op=SUB)
-        widen_next(PAIR, False)
+        table(nc.scalar, 2, 0, EMB_CUT)
+        widen_tiles(1, 0, 2, False)
         transposes(1)
-        widen_next(PAIR, False)
-        nc.scalar.copy(out=tab[:, :, 2, :], in_=cos)
-        widen_next(PAIR, False)
-        widen_next(PAIR, False)
-        widen_next(PAIR, False)
-        widen_next(PAIR, False)
+        widen_tiles(2, 0, 2, False)
+        widen_tiles(3, 0, 2, False)
+        table(nc.scalar, 2, EMB_CUT, R)
+        for n in range(4, 8):
+            widen_tiles(n, 1, 2, False)
         xscale(0)
+        table(nc.vector, 0, EMB_CUT, R)
         quantise(-2)
+        table(nc.vector, 1, EMB_CUT, R)
 
         for s in range(-1, NP - 2):
-            last = s == NP - 3
+            last = s >= 13
             if have(s - 1):
                 v_matmul(s - 1, 0)
                 v_matmul(s - 1, 1)
@@ -346,25 +372,30 @@ def tile_llamaattention_pb_t_w4_kernel(
             kv_copy(s + 1, 0, False)
             if not last:
                 kv_copy(s + 1, 1, False)
-            if s < 2:
-                widen_next(PAIR, False)
-            if s == 0:
-                widen_next(PAIR, False)
+            if s == -1:
+                for n in range(8, 12):
+                    widen_tiles(n, 1, 2, False)
+            if s in (0, 3, 6, 9):
+                widen_tiles(12 + s // 3, 1, 2, False)
             kr_all(s + 1)
-            if s >= 1:
-                widen_next(1, True)
+            if s >= 0 and have(s + 4):
+                widen_tiles(s + 4, 0, 1, True)
             quantise(s)
+            if have(s):
+                rope_sums(s)
+            if last:
+                kv_copy(s + 1, 1, True)
         a, b, c = NP - 3, NP - 2, NP - 1
         v_matmul(a, 0)
         v_matmul(a, 1)
         kc_matmuls(a)
-        kv_copy(b, 1, True)
         kv_matmuls(c, 0)
         kv_matmuls(c, 1)
         v_copy(a, 0, False)
         store_v(a, 0, 1)
         rope_all(b)
         quantise(b)
+        rope_sums(b)
         v_copy(a, 1, False)
         store_v(a, 1, 2)
         kr_all(c)
@@ -377,6 +408,7 @@ def tile_llamaattention_pb_t_w4_kernel(
         kc_matmuls(b)
         rope_all(c)
         quantise(c)
+        rope_sums(c)
         v_copy(b, 0, False)
         store_v(b, 0, 1)
         v_copy(b, 1, False)

@@ -45,7 +45,7 @@ def tile_llamaattention_pb_t_w4_kernel(
         for plane in (s_kv_raw, s_r_raw, s_v, s_k):
             nc.vector.memset(plane[:].bitcast(I32), 0)
 
-        x_cuts = ((0, 0, 2), (0, 2, 4), (0, 4, 8), (0, 8, 16), (1, 0, 8), (1, 8, 16))
+        x_cuts = ((0, 0, 2), (0, 2, 8), (0, 8, 16), (1, 0, 8), (1, 8, 16))
         xb = {}
         for b, r0, r1 in x_cuts:
             xb[b, r0] = keep.tile([P, (r1 - r0) * HID], U8, name="xb%d_%d" % (b, r0))
@@ -58,9 +58,7 @@ def tile_llamaattention_pb_t_w4_kernel(
         w_r_raw = keep.tile([P, 512], U8, name="w_r_raw", align_bytes=64)
         w_r = keep.tile([P, 512], U8, name="w_r", align_bytes=64)
         s_r = keep.tile([P, 256], U8, name="s_r", align_bytes=64)
-        EMB_CUT = 8
-        emb_rows = ((0, EMB_CUT), (EMB_CUT, R))
-        embt = [keep.tile([P, r1 - r0, 2, HALF], BF16, name="embt%d" % r0) for r0, r1 in emb_rows]
+        embt = keep.tile([P, R, 2, HALF], BF16, name="embt")
         tab = keep.tile([P, R, 3, HALF], F32, name="tab")
         ones = keep.tile([P, 1], F32, name="ones")
         nc.vector.memset(ones[:], 1.0)
@@ -81,36 +79,31 @@ def tile_llamaattention_pb_t_w4_kernel(
                     in_=src[0, 4 * q : 4 * q + 4, :].bitcast(I32),
                 )
 
-        def load_emb(i):
-            r0, r1 = emb_rows[i]
+        def load_emb():
             nc.sync.dma_start(
-                out=embt[i][:].rearrange("p r w j -> p r (w j)"),
-                in_=emb[0, 0].rearrange("(p r) c -> p r c", p=P)[:, r0:r1],
+                out=embt[:].rearrange("p r w j -> p r (w j)"),
+                in_=emb[0, 0].rearrange("(p r) c -> p r c", p=P),
             )
 
         load_x(0)
         load_words(nc.sync, w_kv_raw, wkv_words)
-        load_emb(0)
-        load_scales(nc.sync, s_kv_raw, wkv_scales)
         load_x(1)
+        load_scales(nc.sync, s_kv_raw, wkv_scales)
+        load_emb()
         load_x(2)
-        load_emb(1)
-        load_x(3)
         load_words(nc.sync, w_r_raw, wr_words)
         load_scales(nc.sync, s_r_raw, wr_scales)
-        load_x(4)
+        load_x(3)
         load_words(nc.sync, w_v, wv_words)
         load_scales(nc.sync, s_v, wv_scales)
         load_words(nc.sync, w_k, wk_words)
         load_scales(nc.sync, s_k, wk_scales)
-        load_x(5)
+        load_x(4)
         nc.gpsimd.dma_start(out=xsc[:], in_=x_scale.rearrange("a b (p t) -> p (a b t)", t=4))
         make_identity(nc, ident[:])
 
         def table(eng, slot, r0, r1):
-            i = 0 if r0 < EMB_CUT else 1
-            rows = embt[i][:, r0 - emb_rows[i][0] : r1 - emb_rows[i][0]]
-            sin, cos = rows[:, :, 0, :], rows[:, :, 1, :]
+            sin, cos = embt[:, r0:r1, 0, :], embt[:, r0:r1, 1, :]
             if slot == 2:
                 nc.scalar.copy(out=tab[:, r0:r1, 2, :], in_=cos)
             else:
@@ -167,7 +160,7 @@ def tile_llamaattention_pb_t_w4_kernel(
 
         def q_tile(s):
             if s not in qin:
-                qin[s] = work.tile([P, 2, TOK, 4], BF16, name="qin", tag="slot%d" % (s % 4), bufs=1, align_bytes=64)
+                qin[s] = work.tile([P, 2, TOK, 4], BF16, name="qin", bufs=3, align_bytes=64)
             return qin[s]
 
         def xscale(n):
@@ -240,7 +233,7 @@ def tile_llamaattention_pb_t_w4_kernel(
             )
 
         def rope_sums(n):
-            kt[n] = work.tile([P, PAIR, H, HD], F32, name="kt", tag="slot%d" % (n % 4), bufs=1, align_bytes=64)
+            kt[n] = work.tile([P, PAIR, H, HD], F32, name="kt", bufs=5)
             m = prod[n][:].rearrange("p l h c j -> p (l h) c j")
             nc.gpsimd.tensor_tensor(
                 out=kt[n][:].rearrange("p l h (a j) -> p (l h) a j", j=HALF)[:, :, 2:4, :],
@@ -256,6 +249,7 @@ def tile_llamaattention_pb_t_w4_kernel(
         def rope_all(n):
             rope_product(n, 0)
             rope_product(n, 1)
+            rope_sums(n)
 
         def v_matmul(n, l, spare=False):
             codes, scales = operand(n, 1, l)
@@ -327,22 +321,19 @@ def tile_llamaattention_pb_t_w4_kernel(
         widen(0, 1, 2, False)
         transposes(0)
         permute_kv_words()
-        table(nc.vector, 0, 0, EMB_CUT)
-        table(nc.vector, 1, 0, EMB_CUT)
-        permute_kv_scales()
-        table(nc.scalar, 2, 0, EMB_CUT)
         widen_tiles(1, 0, 2, False)
         transposes(1)
         widen_tiles(2, 0, 2, False)
         widen_tiles(3, 0, 2, False)
-        table(nc.scalar, 2, EMB_CUT, R)
+        table(nc.scalar, 2, 0, R)
         for n in range(4, 8):
             widen_tiles(n, 1, 2, False)
-        xscale(0)
-        table(nc.vector, 0, EMB_CUT, R)
-        quantise(-2)
-        table(nc.vector, 1, EMB_CUT, R)
 
+        xscale(0)
+        permute_kv_scales()
+        quantise(-2)
+
+        late_tables = {0: (0, 6, 10), 1: (1, 6, 10), 2: (0, 10, 13), 3: (1, 10, 13), 4: (0, 13, 16), 5: (1, 13, 16)}
         for s in range(-1, NP - 2):
             last = s >= 13
             if have(s - 1):
@@ -366,23 +357,25 @@ def tile_llamaattention_pb_t_w4_kernel(
                 store_k(s - 1)
 
             if s == -1:
+                table(nc.vector, 0, 0, 6)
+                table(nc.vector, 1, 0, 6)
                 permute_r()
             if have(s):
                 rope_all(s)
+                if s in late_tables:
+                    table(nc.gpsimd, *late_tables[s])
             kv_copy(s + 1, 0, False)
             if not last:
                 kv_copy(s + 1, 1, False)
             if s == -1:
                 for n in range(8, 12):
                     widen_tiles(n, 1, 2, False)
-            if s in (0, 3, 6, 9):
-                widen_tiles(12 + s // 3, 1, 2, False)
+            if s in (2, 4, 6, 8):
+                widen_tiles(11 + s // 2, 1, 2, False)
             kr_all(s + 1)
             if s >= 0 and have(s + 4):
                 widen_tiles(s + 4, 0, 1, True)
             quantise(s)
-            if have(s):
-                rope_sums(s)
             if last:
                 kv_copy(s + 1, 1, True)
         a, b, c = NP - 3, NP - 2, NP - 1
@@ -395,7 +388,6 @@ def tile_llamaattention_pb_t_w4_kernel(
         store_v(a, 0, 1)
         rope_all(b)
         quantise(b)
-        rope_sums(b)
         v_copy(a, 1, False)
         store_v(a, 1, 2)
         kr_all(c)
@@ -408,7 +400,6 @@ def tile_llamaattention_pb_t_w4_kernel(
         kc_matmuls(b)
         rope_all(c)
         quantise(c)
-        rope_sums(c)
         v_copy(b, 0, False)
         store_v(b, 0, 1)
         v_copy(b, 1, False)

@@ -59,7 +59,6 @@ def tile_llamaattention_pb_t_w4_kernel(
         w_r = keep.tile([P, 512], U8, name="w_r", align_bytes=64)
         s_r = keep.tile([P, 256], U8, name="s_r", align_bytes=64)
         embt = keep.tile([P, R, 2, HALF], BF16, name="embt")
-        tab = keep.tile([P, R, 3, HALF], F32, name="tab")
         ones = keep.tile([P, 1], F32, name="ones")
         nc.vector.memset(ones[:], 1.0)
         ident = keep.tile([P, P], F32, name="ident")
@@ -158,9 +157,26 @@ def tile_llamaattention_pb_t_w4_kernel(
                         cols = words[:, 256 * l + u : 256 * (l + 1) : 2]
                     nc.tensor.transpose(xT[n][:, u, l, :], cols, ident[:])
 
+        def first_tile(l):
+            bank = psum.tile([P, 2, P], F32, name="xT0", tag=("kcp", "xT")[l], bufs=1)
+            words = xw[0][:].bitcast(F32)
+            for u in range(2):
+                nc.tensor.transpose(bank[:, u, :], words[:, 256 * l + u : 256 * (l + 1) : 2], ident[:])
+            return bank
+
+        def first_xscale(l, bank):
+            nc.vector.tensor_tensor(
+                out=q_tile(-2)[:, 0, l * P : (l + 1) * P].rearrange("p n (u e) -> p n u e", u=2),
+                in0=bank[:].bitcast(BF16).rearrange("p u (n e) -> p n u e", e=2),
+                in1=xsc[:].rearrange("p (u e) -> p u e", u=2).unsqueeze(1).broadcast_to([P, P, 2, 2]),
+                op=MULT,
+            )
+
         def q_tile(s):
             if s not in qin:
-                qin[s] = work.tile([P, 2, TOK, 4], BF16, name="qin", bufs=3, align_bytes=64)
+                qin[s] = work.tile(
+                    [P, 2, TOK, 4], BF16, name="qin", tag="first" if s == -2 else "qin",
+                    bufs=1 if s == -2 else 3, align_bytes=64)
             return qin[s]
 
         def xscale(n):
@@ -263,7 +279,7 @@ def tile_llamaattention_pb_t_w4_kernel(
             )
 
         def kc_matmuls(n):
-            outp[n, 2] = psum.tile([P, PAIR, H * ROT], F32, name="kcp", bufs=1)
+            outp[n, 2] = psum.tile([P, PAIR, H * ROT], F32, name="kcp", tag="kcp", bufs=1)
             for l in range(PAIR):
                 codes, scales = operand(n, 1, l)
                 nc.tensor.matmul_mx(
@@ -319,21 +335,25 @@ def tile_llamaattention_pb_t_w4_kernel(
 
         widen(0, 0, 1, True)
         widen(0, 1, 2, False)
-        transposes(0)
+        banks0 = [first_tile(l) for l in range(PAIR)]
         permute_kv_words()
         widen_tiles(1, 0, 2, False)
         transposes(1)
         widen_tiles(2, 0, 2, False)
         widen_tiles(3, 0, 2, False)
+
+        for l in range(PAIR):
+            first_xscale(l, banks0[l])
+        permute_kv_scales()
+        quantise(-2)
+        tab = work.tile([P, R, 3, HALF], F32, name="tab", tag="first", bufs=1, align_bytes=64)
+        for r0, r1 in ((0, 6), (6, R)):
+            table(nc.gpsimd, 0, r0, r1)
+            table(nc.gpsimd, 1, r0, r1)
         table(nc.scalar, 2, 0, R)
         for n in range(4, 8):
             widen_tiles(n, 1, 2, False)
 
-        xscale(0)
-        permute_kv_scales()
-        quantise(-2)
-
-        late_tables = {0: (0, 6, 10), 1: (1, 6, 10), 2: (0, 10, 13), 3: (1, 10, 13), 4: (0, 13, 16), 5: (1, 13, 16)}
         for s in range(-1, NP - 2):
             last = s >= 13
             if have(s - 1):
@@ -357,13 +377,9 @@ def tile_llamaattention_pb_t_w4_kernel(
                 store_k(s - 1)
 
             if s == -1:
-                table(nc.vector, 0, 0, 6)
-                table(nc.vector, 1, 0, 6)
                 permute_r()
             if have(s):
                 rope_all(s)
-                if s in late_tables:
-                    table(nc.gpsimd, *late_tables[s])
             kv_copy(s + 1, 0, False)
             if not last:
                 kv_copy(s + 1, 1, False)
@@ -372,8 +388,11 @@ def tile_llamaattention_pb_t_w4_kernel(
                     widen_tiles(n, 1, 2, False)
             if s in (2, 4, 6, 8):
                 widen_tiles(11 + s // 2, 1, 2, False)
+            if s == 0:
+                for n in (4,):
+                    widen_tiles(n, 0, 1, False)
             kr_all(s + 1)
-            if s >= 0 and have(s + 4):
+            if have(s + 4) and (s + 4, 0) in tiles:
                 widen_tiles(s + 4, 0, 1, True)
             quantise(s)
             if last:

@@ -12,7 +12,6 @@ FP8 = mybir.dt.float8_e4m3fn
 FP8X4 = mybir.dt.float8_e4m3fn_x4
 FP4X4 = mybir.dt.float4_e2m1fn_x4
 ADD = mybir.AluOpType.add
-SUB = mybir.AluOpType.subtract
 MULT = mybir.AluOpType.mult
 
 B, S, H, HD, HID, LAT = 2, 2048, 4, 128, 512, 512
@@ -24,7 +23,6 @@ FLOPS = 2 * B * S * HID * (LAT + H * ROT + H * HD + H * ROT)
 PAIR = 2
 TOK = PAIR * P
 NP = B * R // PAIR
-HEAD_WIDENS = 7
 
 
 def tile_llamaattention_pb_t_w4_kernel(
@@ -39,13 +37,13 @@ def tile_llamaattention_pb_t_w4_kernel(
         ctx.enter_context(tc.manual_schedule())
 
         s_kv_raw = keep.tile([P, 512], U8, name="s_kv_raw", align_bytes=64)
-        s_r_raw = keep.tile([P, 256], U8, name="s_r_raw", align_bytes=64)
+        s_r = keep.tile([P, 256], U8, name="s_r", align_bytes=64)
         s_v = keep.tile([P, 512], U8, name="s_v", align_bytes=64)
         s_k = keep.tile([P, 256], U8, name="s_k", align_bytes=64)
-        for plane in (s_kv_raw, s_r_raw, s_v, s_k):
+        for plane in (s_kv_raw, s_r, s_v, s_k):
             nc.vector.memset(plane[:].bitcast(I32), 0)
 
-        x_cuts = ((0, 0, 2), (0, 2, 8), (0, 8, 16), (1, 0, 8), (1, 8, 16))
+        x_cuts = ((0, 0, 2), (0, 2, 4), (0, 4, 8), (0, 8, 12), (0, 12, 16), (1, 0, 8), (1, 8, 16))
         xb = {}
         for b, r0, r1 in x_cuts:
             xb[b, r0] = keep.tile([P, (r1 - r0) * HID], U8, name="xb%d_%d" % (b, r0))
@@ -55,12 +53,9 @@ def tile_llamaattention_pb_t_w4_kernel(
         s_kv = keep.tile([P, 512], U8, name="s_kv", align_bytes=64)
         w_v = keep.tile([P, 1024], U8, name="w_v", align_bytes=64)
         w_k = keep.tile([P, 512], U8, name="w_k", align_bytes=64)
-        w_r_raw = keep.tile([P, 512], U8, name="w_r_raw", align_bytes=64)
         w_r = keep.tile([P, 512], U8, name="w_r", align_bytes=64)
-        s_r = keep.tile([P, 256], U8, name="s_r", align_bytes=64)
         embt = keep.tile([P, R, 2, HALF], BF16, name="embt")
-        ones = keep.tile([P, 1], F32, name="ones")
-        nc.vector.memset(ones[:], 1.0)
+        tab = keep.tile([P, R, 2, 2, HALF], BF16, name="tab")
         ident = keep.tile([P, P], F32, name="ident")
 
         def load_x(i):
@@ -68,145 +63,91 @@ def tile_llamaattention_pb_t_w4_kernel(
             rows = x_bytes[b].rearrange("(p r) k -> p r k", p=P)[:, r0:r1, :]
             nc.sync.dma_start(out=xb[b, r0][:].rearrange("p (r k) -> p r k", k=HID), in_=rows)
 
-        def load_words(eng, tile, src):
-            eng.dma_start(out=tile[:].bitcast(I32), in_=src[0].bitcast(I32))
+        def load_words(tile, src):
+            nc.sync.dma_start(out=tile[:].bitcast(I32), in_=src[0].bitcast(I32))
 
-        def load_scales(eng, plane, src):
+        def load_scales(plane, src):
             for q in range(4):
-                eng.dma_start(
+                nc.sync.dma_start(
                     out=plane[32 * q : 32 * q + 4, :].bitcast(I32),
                     in_=src[0, 4 * q : 4 * q + 4, :].bitcast(I32),
                 )
 
-        def load_emb():
-            nc.sync.dma_start(
-                out=embt[:].rearrange("p r w j -> p r (w j)"),
-                in_=emb[0, 0].rearrange("(p r) c -> p r c", p=P),
-            )
-
-        load_x(0)
-        load_words(nc.sync, w_kv_raw, wkv_words)
-        load_x(1)
-        load_scales(nc.sync, s_kv_raw, wkv_scales)
-        load_emb()
-        load_x(2)
-        load_words(nc.sync, w_r_raw, wr_words)
-        load_scales(nc.sync, s_r_raw, wr_scales)
-        load_x(3)
-        load_words(nc.sync, w_v, wv_words)
-        load_scales(nc.sync, s_v, wv_scales)
-        load_words(nc.sync, w_k, wk_words)
-        load_scales(nc.sync, s_k, wk_scales)
-        load_x(4)
-        nc.gpsimd.dma_start(out=xsc[:], in_=x_scale.rearrange("a b (p t) -> p (a b t)", t=4))
         make_identity(nc, ident[:])
+        load_x(0)
+        load_x(1)
+        load_words(w_kv_raw, wkv_words)
+        nc.sync.dma_start(out=xsc[:], in_=x_scale.rearrange("a b (p t) -> p (a b t)", t=4))
+        load_x(2)
+        load_x(3)
+        load_scales(s_kv_raw, wkv_scales)
+        nc.sync.dma_start(
+            out=embt[:].rearrange("p r w j -> p r (w j)"),
+            in_=emb[0, 0].rearrange("(p r) c -> p r c", p=P),
+        )
+        load_x(4)
+        load_words(w_r, wr_words)
+        load_scales(s_r, wr_scales)
+        load_words(w_v, wv_words)
+        load_scales(s_v, wv_scales)
+        load_x(5)
+        load_words(w_k, wk_words)
+        load_scales(s_k, wk_scales)
+        load_x(6)
 
-        def table(eng, slot, r0, r1):
-            sin, cos = embt[:, r0:r1, 0, :], embt[:, r0:r1, 1, :]
-            if slot == 2:
-                nc.scalar.copy(out=tab[:, r0:r1, 2, :], in_=cos)
-            else:
-                eng.tensor_tensor(out=tab[:, r0:r1, slot, :], in0=cos, in1=sin, op=(ADD, SUB)[slot])
-
-        xw, xT, qin, quant, kvp, krp, kt, vt, outp, prod = {}, {}, {}, {}, {}, {}, {}, {}, {}, {}
-
-        tiles = [(n, l) for n in range(1, NP) for l in range(PAIR)]
-
-        sorted_words = set()
+        xw, xT, qx, qk, xq, kq, kvp, krp, kt, vt, vp, kcp, prod = ({}, {}, {}, {}, {}, {}, {}, {}, {}, {}, {}, {}, {})
 
         def where(n):
             return n // (R // PAIR), PAIR * (n % (R // PAIR))
 
-        def have(n):
-            return 0 <= n < NP
-
-        def copy_on(on_vector, out, in_):
-            if on_vector == "gpsimd":
-                nc.gpsimd.tensor_copy(out=out, in_=in_)
-            elif on_vector:
-                nc.vector.tensor_copy(out=out, in_=in_)
-            else:
+        def copy_on(eng, out, in_):
+            if eng is nc.scalar:
                 nc.scalar.copy(out=out, in_=in_)
+            else:
+                eng.tensor_copy(out=out, in_=in_)
 
-        def widen(n, l0, l1, on_vector):
+        def widen(eng, n, l0, l1, tag="xw"):
             b, r = where(n)
             r0 = max(c[1] for c in x_cuts if c[0] == b and c[1] <= r)
-            if n not in xw:
-                xw[n] = work.tile([P, PAIR * HID], BF16, name="xw", bufs=16)
+            wide = work.tile([P, (l1 - l0) * HID], BF16, name="xw", tag=tag, bufs=12 if tag == "xw" else 1, align_bytes=64)
+            for l in range(l0, l1):
+                xw[n, l] = wide[:, (l - l0) * HID : (l - l0 + 1) * HID]
             src = xb[b, r0][:, (r - r0 + l0) * HID : (r - r0 + l1) * HID].bitcast(FP8)
-            if on_vector and n > 0:
-                sorted_words.add((n, l0))
-                nc.vector.tensor_scalar(
-                    out=xw[n][:, l0 * HID : l1 * HID].rearrange("p (u m e) -> p m u e", u=2, e=2),
-                    in0=src.rearrange("p (m u e) -> p m u e", u=2, e=2), scalar1=ones[:], scalar2=None, op0=MULT)
-            else:
-                copy_on(on_vector, xw[n][:, l0 * HID : l1 * HID], src)
+            copy_on(eng, wide[:], src)
 
-        def transposes(n):
-            assert (n, 0) not in tiles and (n, 1) not in tiles
-            if n in (1, 2):
-                xT[n] = psum.tile([P, 2, PAIR, P], F32, name="xTv", tag="vp", bufs=2)
-            else:
-                xT[n] = psum.tile([P, 2, PAIR, P], F32, name="xT", tag="xT", bufs=1)
-            words = xw[n][:].bitcast(F32)
-            for l in range(PAIR):
+        def transposes(n, l0, l1, tag):
+            bank = psum.tile([P, 2, l1 - l0, P], F32, name="xT", tag=tag, bufs=2 if tag in ("xT", "kvp", "vp") else 1)
+            xT[n, l0] = bank
+            for l in range(l0, l1):
+                words = xw[n, l].bitcast(F32)
                 for u in range(2):
-                    if (n, l) in sorted_words:
-                        cols = words[:, 256 * l + P * u : 256 * l + P * (u + 1)]
-                    else:
-                        cols = words[:, 256 * l + u : 256 * (l + 1) : 2]
-                    nc.tensor.transpose(xT[n][:, u, l, :], cols, ident[:])
+                    nc.tensor.transpose(bank[:, u, l - l0, :], words[:, u : 256 : 2], ident[:])
 
-        def first_tile(l):
-            bank = psum.tile([P, 2, P], F32, name="xT0", tag=("kcp", "xT")[l], bufs=1)
-            words = xw[0][:].bitcast(F32)
-            for u in range(2):
-                nc.tensor.transpose(bank[:, u, :], words[:, 256 * l + u : 256 * (l + 1) : 2], ident[:])
-            return bank
-
-        def first_xscale(l, bank):
+        def xscale(n, l0, l1):
+            if n not in qx:
+                qx[n] = work.tile([P, TOK, 4], BF16, name="qx", tag="qx%d" % n, bufs=1, align_bytes=64)
             nc.vector.tensor_tensor(
-                out=q_tile(-2)[:, 0, l * P : (l + 1) * P].rearrange("p n (u e) -> p n u e", u=2),
-                in0=bank[:].bitcast(BF16).rearrange("p u (n e) -> p n u e", e=2),
-                in1=xsc[:].rearrange("p (u e) -> p u e", u=2).unsqueeze(1).broadcast_to([P, P, 2, 2]),
+                out=qx[n][:, l0 * P : l1 * P].rearrange("p n (u e) -> p n u e", u=2),
+                in0=xT[n, l0][:].bitcast(BF16).rearrange("p u l (n e) -> p (l n) u e", e=2),
+                in1=xsc[:].rearrange("p (u e) -> p u e", u=2).unsqueeze(1).broadcast_to([P, (l1 - l0) * P, 2, 2]),
                 op=MULT,
             )
 
-        def q_tile(s):
-            if s not in qin:
-                qin[s] = work.tile(
-                    [P, 2, TOK, 4], BF16, name="qin", tag="first" if s == -2 else "qin",
-                    bufs=1 if s == -2 else 3, align_bytes=64)
-            return qin[s]
-
-        def xscale(n):
-            nc.vector.tensor_tensor(
-                out=q_tile(n - 2)[:, 0].rearrange("p n (u e) -> p n u e", u=2),
-                in0=xT[n][:].bitcast(BF16).rearrange("p u l (n e) -> p (l n) u e", e=2),
-                in1=xsc[:].rearrange("p (u e) -> p u e", u=2).unsqueeze(1).broadcast_to([P, TOK, 2, 2]),
-                op=MULT,
-            )
-
-        def quantise(s):
-            codes = work.tile([P, 2, TOK], U32, name="codes", bufs=4, align_bytes=64)
-            scales = work.tile([P, 2, TOK], U8, name="scales", bufs=4, align_bytes=64)
-            quant[s] = (codes, scales)
-            lo = 0 if have(s + 2) else 1
-            hi = 2 if have(s) else 1
+        def quantise(src, dst, n, name):
+            codes = work.tile([P, TOK], U32, name=name + "_codes", bufs=3, align_bytes=64)
+            scales = work.tile([P, TOK], U8, name=name + "_scales", bufs=3, align_bytes=64)
+            dst[n] = (codes, scales)
             nc.vector.quantize_mx(
-                out=codes[:, lo:hi].rearrange("p a n -> p (a n)").bitcast(FP8X4),
-                scales=scales[:, lo:hi].rearrange("p a n -> p (a n)"),
-                in_=q_tile(s)[:, lo:hi].rearrange("p a n t -> p (a n t)"),
-            )
+                out=codes[:].bitcast(FP8X4), scales=scales[:], in_=src[n][:].rearrange("p n t -> p (n t)"))
 
-        def operand(s, a, l):
-            codes, scales = quant[s]
+        def operand(quant, l):
+            codes, scales = quant
             cols = slice(l * P, (l + 1) * P)
-            return codes[:, a, cols].bitcast(FP8X4), scales[:, a, cols]
+            return codes[:, cols].bitcast(FP8X4), scales[:, cols]
 
         def kv_matmuls(n, l):
-            codes, scales = operand(n - 2, 0, l)
-            kvp[n, l] = psum.tile([P, 4, P], F32, name="kvp", bufs=2)
+            codes, scales = operand(xq[n], l)
+            kvp[n, l] = psum.tile([P, 4, P], F32, name="kvp", tag="kvp", bufs=2)
             for t in range(4):
                 nc.tensor.matmul_mx(
                     kvp[n, l][:, t, :],
@@ -216,99 +157,88 @@ def tile_llamaattention_pb_t_w4_kernel(
                     start=True, stop=True,
                 )
 
-        def kv_copy(n, l, on_vector):
+        def kv_copy(eng, n, l):
+            if n not in qk:
+                qk[n] = work.tile([P, TOK, 4], BF16, name="qk", tag="qk0" if n == 0 else "qk",
+                                  bufs=1 if n == 0 else 2, align_bytes=64)
             copy_on(
-                on_vector,
-                q_tile(n)[:, 1, l * P : (l + 1) * P, :].rearrange("p (c i) t -> p c t i", i=2),
+                eng,
+                qk[n][:, l * P : (l + 1) * P, :].rearrange("p (c i) t -> p c t i", i=2),
                 kvp[n, l][:].rearrange("p t (c i) -> p c t i", i=2),
             )
 
-        def kr_matmuls(n, l):
-            codes, scales = operand(n - 2, 0, l)
-            krp[n, l] = psum.tile([P, 3, H * HALF], F32, name="krp", tag="krp", bufs=2)
-            for out, lo, hi, start, stop in (
-                (krp[n, l][:, 0:2].rearrange("p c m -> p (c m)"), 0, 256, True, True),
-                (krp[n, l][:, 2], 0, 128, True, False),
-                (krp[n, l][:, 2], 128, 256, False, True),
-            ):
+        def kr_matmuls(n, tag="krp"):
+            krp[n] = psum.tile([P, PAIR, H * ROT], F32, name="krp", tag=tag, bufs=1 if tag == "krp" else 2)
+            for l in range(PAIR):
+                codes, scales = operand(xq[n], l)
                 nc.tensor.matmul_mx(
-                    out, lhsT=codes, lhsT_scale=scales,
-                    rhs=w_r[:, 2 * lo : 2 * hi].bitcast(FP4X4), rhs_scale=s_r[:, lo:hi],
-                    start=start, stop=stop,
+                    krp[n][:, l], lhsT=codes, lhsT_scale=scales,
+                    rhs=w_r[:].bitcast(FP4X4), rhs_scale=s_r[:], start=True, stop=True,
                 )
 
-        def rope_product(n, l):
+        def rope_products(n, l0=0, l1=PAIR):
             b, r = where(n)
-            if l == 0:
-                prod[n] = work.tile([P, PAIR, H, 3, HALF], F32, name="prod", bufs=2)
+            if l0 == 0:
+                prod[n] = work.tile([P, PAIR, H, 2, ROT], F32, name="prod", bufs=3)
+            shape = [P, l1 - l0, H, 2, ROT]
             nc.vector.tensor_tensor(
-                out=prod[n][:, l].rearrange("p h c j -> p c h j"),
-                in0=krp[n, l][:].rearrange("p c (h j) -> p c h j", h=H),
-                in1=tab[:, r + l].unsqueeze(2).broadcast_to([P, 3, H, HALF]),
+                out=prod[n][:, l0:l1],
+                in0=krp[n][:, l0:l1].rearrange("p l (h d) -> p l h d", h=H).unsqueeze(3).broadcast_to(shape),
+                in1=tab[:, r + l0 : r + l1].rearrange("p l a c j -> p l a (c j)").unsqueeze(2).broadcast_to(shape),
                 op=MULT,
             )
 
-        def rope_sums(n):
-            kt[n] = work.tile([P, PAIR, H, HD], F32, name="kt", bufs=5)
-            m = prod[n][:].rearrange("p l h c j -> p (l h) c j")
-            nc.gpsimd.tensor_tensor(
-                out=kt[n][:].rearrange("p l h (a j) -> p (l h) a j", j=HALF)[:, :, 2:4, :],
-                in0=m[:, :, 2:3, :].broadcast_to([P, PAIR * H, 2, HALF]),
-                in1=m[:, :, 0:2, :],
-                op=SUB,
+        def k_tile(n):
+            if n not in kt:
+                kt[n] = work.tile([P, PAIR, H, HD], F32, name="kt", bufs=4)
+            return kt[n]
+
+        def rope_sums(eng, n, l0=0, l1=PAIR):
+            m = prod[n][:, l0:l1].rearrange("p l h a (c j) -> p (l h) a c j", c=2)
+            eng.tensor_tensor(
+                out=k_tile(n)[:, l0:l1].rearrange("p l h (a j) -> p (l h) a j", j=HALF)[:, :, 2:4, :],
+                in0=m[:, :, :, 0, :], in1=m[:, :, :, 1, :], op=ADD,
             )
 
-        def kr_all(n):
-            kr_matmuls(n, 0)
-            kr_matmuls(n, 1)
-
-        def rope_all(n):
-            rope_product(n, 0)
-            rope_product(n, 1)
-            rope_sums(n)
-
-        def v_matmul(n, l, spare=False):
-            codes, scales = operand(n, 1, l)
-            if spare:
-                outp[n, l] = psum.tile([P, 512], F32, name="vx", tag="xT", bufs=1)
-            else:
-                outp[n, l] = psum.tile([P, 512], F32, name="vp", tag="vp", bufs=2)
+        def v_matmul(n, l):
+            codes, scales = operand(kq[n], l)
+            vp[n, l] = psum.tile([P, 512], F32, name="vp", tag="vp", bufs=2)
             nc.tensor.matmul_mx(
-                outp[n, l][:], lhsT=codes, lhsT_scale=scales,
+                vp[n, l][:], lhsT=codes, lhsT_scale=scales,
                 rhs=w_v[:].bitcast(FP4X4), rhs_scale=s_v[:], start=True, stop=True,
             )
 
         def kc_matmuls(n):
-            outp[n, 2] = psum.tile([P, PAIR, H * ROT], F32, name="kcp", tag="kcp", bufs=1)
+            kcp[n] = psum.tile([P, PAIR, H * ROT], F32, name="kcp", tag="kcp", bufs=1)
             for l in range(PAIR):
-                codes, scales = operand(n, 1, l)
+                codes, scales = operand(kq[n], l)
                 nc.tensor.matmul_mx(
-                    outp[n, 2][:, l], lhsT=codes, lhsT_scale=scales,
+                    kcp[n][:, l], lhsT=codes, lhsT_scale=scales,
                     rhs=w_k[:].bitcast(FP4X4), rhs_scale=s_k[:], start=True, stop=True,
                 )
 
-        def v_copy(n, l, on_vector):
+        def v_copy(eng, n, l):
             if l == 0:
                 vt[n] = work.tile([P, PAIR, H * HD], F32, name="vt", bufs=4)
-            copy_on(on_vector, vt[n][:, l, :], outp[n, l][:])
+            copy_on(eng, vt[n][:, l, :], vp[n, l][:])
 
-        def kc_copy(n, on_vector, l0=0, l1=PAIR):
+        def kc_copy(eng, n):
             copy_on(
-                on_vector,
-                kt[n][:, l0:l1].rearrange("p l h d -> p (l h) d")[:, :, 0:ROT],
-                outp[n, 2][:, l0:l1].rearrange("p l (h d) -> p (l h) d", h=H),
+                eng,
+                k_tile(n)[:].rearrange("p l h d -> p (l h) d")[:, :, 0:ROT],
+                kcp[n][:].rearrange("p l (h d) -> p (l h) d", h=H),
             )
+
+        def store(out, tile, n, l0, l1):
+            b, r = where(n)
+            rows = out[b].rearrange("(p r) h d -> p r (h d)", p=P)
+            nc.sync.dma_start(out=rows[:, r + l0 : r + l1, :], in_=tile[:, l0:l1])
 
         def store_v(n, l0=0, l1=PAIR):
             store(v_out, vt[n], n, l0, l1)
 
         def store_k(n, l0=0, l1=PAIR):
             store(k_out, kt[n][:].rearrange("p l h d -> p l (h d)"), n, l0, l1)
-
-        def store(out, tile, n, l0, l1):
-            b, r = where(n)
-            rows = out[b].rearrange("(p r) h d -> p r (h d)", p=P)
-            nc.sync.dma_start(out=rows[:, r + l0 : r + l1, :], in_=tile[:, l0:l1])
 
         def permute_kv_words():
             nc.vector.tensor_copy(
@@ -320,118 +250,111 @@ def tile_llamaattention_pb_t_w4_kernel(
                 out=s_kv[:].rearrange("p (t m) -> p t m", t=4),
                 in_=s_kv_raw[:].rearrange("p (m t) -> p t m", t=4))
 
-        def permute_r():
-            for dst, src in ((w_r, w_r_raw), (s_r, s_r_raw)):
-                for a in range(2):
-                    nc.vector.tensor_copy(
-                        out=dst[:].bitcast(I32).rearrange("p (a h c) -> p a h c", a=2, h=H)[:, 1 - a],
-                        in_=src[:].bitcast(I32).rearrange("p (h a c) -> p a h c", a=2, h=H)[:, a])
+        def table():
+            nc.vector.tensor_copy(out=tab[:, :, 1], in_=embt[:])
+            nc.vector.tensor_copy(out=tab[:, :, 0, 0], in_=embt[:, :, 1])
+            nc.vector.tensor_scalar(out=tab[:, :, 0, 1], in0=embt[:, :, 0], scalar1=-1.0, scalar2=None, op0=MULT)
 
+        V, A, G = nc.vector, nc.scalar, nc.gpsimd
+        late = [(n, l) for n in range(10, NP) for l in range(PAIR)]
 
-        def widen_tiles(n, l0, l1, on_vector):
-            for l in range(l0, l1):
-                tiles.remove((n, l))
-            widen(n, l0, l1, on_vector)
-
-        widen(0, 0, 1, True)
-        widen(0, 1, 2, False)
-        banks0 = [first_tile(l) for l in range(PAIR)]
+        widen(V, 0, 0, 1)
+        widen(A, 0, 1, 2)
+        transposes(0, 0, 1, "kcp")
+        transposes(0, 1, 2, "xT")
+        widen(A, 1, 0, 2)
         permute_kv_words()
-        widen_tiles(1, 0, 2, False)
-        transposes(1)
-        widen_tiles(2, 0, 2, False)
-        widen_tiles(3, 0, 2, False)
-
-        for l in range(PAIR):
-            first_xscale(l, banks0[l])
+        transposes(1, 0, 2, "xT")
+        widen(A, 2, 0, 2)
+        widen(G, 3, 0, 1)
+        widen(A, 3, 1, 2)
+        xscale(0, 0, 1)
+        xscale(0, 1, 2)
+        transposes(2, 0, 2, "vp")
+        widen(A, 4, 0, 2)
+        quantise(qx, xq, 0, "x")
         permute_kv_scales()
-        quantise(-2)
-        tab = work.tile([P, R, 3, HALF], F32, name="tab", tag="first", bufs=1, align_bytes=64)
-        for r0, r1 in ((0, 6), (6, R)):
-            table(nc.gpsimd, 0, r0, r1)
-            table(nc.gpsimd, 1, r0, r1)
-        table(nc.scalar, 2, 0, R)
-        for n in range(4, 8):
-            widen_tiles(n, 1, 2, False)
+        widen(G, 5, 0, 1, "qx0")
+        widen(A, 5, 1, 2)
+        widen(A, 6, 0, 2)
+        xscale(1, 0, 2)
+        kv_matmuls(0, 0)
+        kv_matmuls(0, 1)
+        kr_matmuls(0)
+        table()
+        quantise(qx, xq, 1, "x")
+        widen(G, 7, 0, 1, "qx1")
+        kv_copy(A, 0, 0)
+        kv_copy(A, 0, 1)
+        widen(A, 7, 1, 2)
+        kv_matmuls(1, 0)
+        kv_matmuls(1, 1)
+        transposes(3, 0, 2, "xT")
+        kv_copy(A, 1, 0)
+        kv_copy(A, 1, 1)
+        widen(A, 8, 1, 2)
 
-        for s in range(-1, NP - 2):
-            last = s >= 13
-            if have(s - 1):
-                v_matmul(s - 1, 0)
-                v_matmul(s - 1, 1)
-                kc_matmuls(s - 1)
-            xscale(s + 2)
-            if s < 0:
-                transposes(s + 3)
-            kv_matmuls(s + 1, 0)
-            kv_matmuls(s + 1, 1)
-            if s >= 0 and have(s + 3):
-                transposes(s + 3)
-            if have(s - 1):
-                v_copy(s - 1, 0, False)
-                if s >= 12:
-                    store_v(s - 1, 0, 1)
-                v_copy(s - 1, 1, False)
-                store_v(s - 1, 1 if s >= 12 else 0, 2)
-                kc_copy(s - 1, False)
-                store_k(s - 1)
+        def outputs(n):
+            v_matmul(n, 0)
+            v_matmul(n, 1)
+            kc_matmuls(n)
 
-            if s == -1:
-                permute_r()
-            if have(s):
-                rope_all(s)
-            kv_copy(s + 1, 0, False)
-            if not last:
-                kv_copy(s + 1, 1, False)
-            if s == -1:
-                for n in range(8, 12):
-                    widen_tiles(n, 1, 2, False)
-            if s in (2, 4, 6, 8):
-                widen_tiles(11 + s // 2, 1, 2, False)
-            if s == 0:
-                for n in (4,):
-                    widen_tiles(n, 0, 1, False)
-            kr_all(s + 1)
-            if have(s + 4) and (s + 4, 0) in tiles:
-                widen_tiles(s + 4, 0, 1, True)
-            quantise(s)
-            if last:
-                kv_copy(s + 1, 1, True)
-        a, b, c = NP - 3, NP - 2, NP - 1
-        v_matmul(a, 0)
-        v_matmul(a, 1)
-        kc_matmuls(a)
-        kv_matmuls(c, 0)
-        kv_matmuls(c, 1)
-        v_copy(a, 0, False)
-        store_v(a, 0, 1)
-        rope_all(b)
-        quantise(b)
-        v_copy(a, 1, False)
-        store_v(a, 1, 2)
-        kr_all(c)
-        kc_copy(a, True)
+        for m in range(2, NP):
+            xscale(m, 0, 2)
+            if m == 2:
+                quantise(qk, kq, 0, "kv")
+                widen(G, 8, 0, 1, "qk0")
+                outputs(0)
+                v_copy(A, 0, 0)
+                store_v(0, 0, 1)
+                v_copy(A, 0, 1)
+                store_v(0, 1, 2)
+                kc_copy(A, 0)
+            rope_products(m - 2)
+            quantise(qx, xq, m, "x")
+            quantise(qk, kq, m - 1, "kv")
+            if m - 2 < len(late):
+                widen(G, late[m - 2][0], late[m - 2][1], late[m - 2][1] + 1, "qx%d" % m)
+            rope_sums(G, m - 2)
+            store_k(m - 2)
+            if m < NP - 1:
+                kr_matmuls(m - 1)
+            kv_matmuls(m, 0)
+            kv_matmuls(m, 1)
+            if m == NP - 1:
+                break
+            kv_copy(A, m, 0)
+            kv_copy(A, m, 1)
+            outputs(m - 1)
+            if m + 2 < NP:
+                transposes(m + 2, 0, 2, "xT")
+            if m == NP - 2:
+                kr_matmuls(m, "xT")
+            v_copy(A, m - 1, 0)
+            v_copy(A, m - 1, 1)
+            store_v(m - 1)
+            kc_copy(A, m - 1)
+            if m == 2:
+                widen(V, 9, 0, 2)
+        a, b = NP - 2, NP - 1
+        kr_matmuls(b)
+        outputs(a)
+        rope_products(a, 0, 1)
+        kv_copy(V, b, 0)
+        kv_copy(A, b, 1)
+        rope_products(a, 1, 2)
+        quantise(qk, kq, b, "kv")
+        rope_sums(G, a)
+        rope_products(b)
+        v_copy(A, a, 0)
+        v_copy(A, a, 1)
+        store_v(a)
+        kc_copy(A, a)
         store_k(a)
-        kv_copy(c, 0, False)
-        kv_copy(c, 1, True)
-        v_matmul(b, 0)
-        v_matmul(b, 1)
-        kc_matmuls(b)
-        rope_all(c)
-        quantise(c)
-        v_copy(b, 0, False)
-        store_v(b, 0, 1)
-        v_copy(b, 1, False)
-        store_v(b, 1, 2)
-        v_matmul(c, 0, True)
-        kc_copy(b, True)
+        rope_sums(G, b)
+        outputs(b)
+        v_copy(A, b, 0)
+        v_copy(V, b, 1)
+        store_v(b)
+        kc_copy(A, b)
         store_k(b)
-        v_matmul(c, 1)
-        kc_matmuls(c)
-        v_copy(c, 0, False)
-        store_v(c, 0, 1)
-        v_copy(c, 1, True)
-        store_v(c, 1, 2)
-        kc_copy(c, False)
-        store_k(c, 0, 1)
-        store_k(c, 1, 2)

@@ -43,7 +43,7 @@ def tile_llamaattention_pb_t_w4_kernel(
         for plane in (s_kv_raw, s_r, s_v, s_k):
             nc.vector.memset(plane[:].bitcast(I32), 0)
 
-        x_cuts = ((0, 0, 2), (0, 2, 4), (0, 4, 8), (0, 8, 12), (0, 12, 16), (1, 0, 8), (1, 8, 16))
+        x_cuts = ((0, 0, 2), (0, 2, 4), (0, 4, 8), (0, 8, 12), (0, 12, 16), (1, 0, 4), (1, 4, 12), (1, 12, 16))
         xb = {}
         for b, r0, r1 in x_cuts:
             xb[b, r0] = keep.tile([P, (r1 - r0) * HID], U8, name="xb%d_%d" % (b, r0))
@@ -79,21 +79,22 @@ def tile_llamaattention_pb_t_w4_kernel(
         load_words(w_kv_raw, wkv_words)
         nc.sync.dma_start(out=xsc[:], in_=x_scale.rearrange("a b (p t) -> p (a b t)", t=4))
         load_x(2)
-        load_x(3)
         load_scales(s_kv_raw, wkv_scales)
+        load_x(3)
+        load_x(4)
         nc.sync.dma_start(
             out=embt[:].rearrange("p r w j -> p r (w j)"),
             in_=emb[0, 0].rearrange("(p r) c -> p r c", p=P),
         )
-        load_x(4)
         load_words(w_r, wr_words)
         load_scales(s_r, wr_scales)
+        load_x(5)
         load_words(w_v, wv_words)
         load_scales(s_v, wv_scales)
-        load_x(5)
         load_words(w_k, wk_words)
         load_scales(s_k, wk_scales)
         load_x(6)
+        load_x(7)
 
         xw, xT, qx, qk, xq, kq, kvp, krp, kt, vt, vp, kcp, prod = ({}, {}, {}, {}, {}, {}, {}, {}, {}, {}, {}, {}, {})
 
@@ -109,7 +110,7 @@ def tile_llamaattention_pb_t_w4_kernel(
         def widen(eng, n, l0, l1, tag="xw"):
             b, r = where(n)
             r0 = max(c[1] for c in x_cuts if c[0] == b and c[1] <= r)
-            wide = work.tile([P, (l1 - l0) * HID], BF16, name="xw", tag=tag, bufs=12 if tag == "xw" else 1, align_bytes=64)
+            wide = work.tile([P, (l1 - l0) * HID], BF16, name="xw", tag=tag, bufs=16 if tag == "xw" else 1, align_bytes=64)
             for l in range(l0, l1):
                 xw[n, l] = wide[:, (l - l0) * HID : (l - l0 + 1) * HID]
             src = xb[b, r0][:, (r - r0 + l0) * HID : (r - r0 + l1) * HID].bitcast(FP8)
@@ -190,7 +191,10 @@ def tile_llamaattention_pb_t_w4_kernel(
 
         def k_tile(n):
             if n not in kt:
-                kt[n] = work.tile([P, PAIR, H, HD], F32, name="kt", bufs=4)
+                if n + 2 < NP:
+                    kt[n] = work.tile([P, PAIR, H, HD], F32, name="kt", tag="qx%d" % (n + 2), bufs=1, align_bytes=64)
+                else:
+                    kt[n] = work.tile([P, PAIR, H, HD], F32, name="kt", bufs=2)
             return kt[n]
 
         def rope_sums(eng, n, l0=0, l1=PAIR):
@@ -250,13 +254,15 @@ def tile_llamaattention_pb_t_w4_kernel(
                 out=s_kv[:].rearrange("p (t m) -> p t m", t=4),
                 in_=s_kv_raw[:].rearrange("p (m t) -> p t m", t=4))
 
-        def table():
-            nc.vector.tensor_copy(out=tab[:, :, 1], in_=embt[:])
-            nc.vector.tensor_copy(out=tab[:, :, 0, 0], in_=embt[:, :, 1])
-            nc.vector.tensor_scalar(out=tab[:, :, 0, 1], in0=embt[:, :, 0], scalar1=-1.0, scalar2=None, op0=MULT)
+        def table(a):
+            if a == 1:
+                nc.vector.tensor_copy(out=tab[:, :, 1], in_=embt[:])
+            else:
+                nc.vector.tensor_copy(out=tab[:, :, 0, 0], in_=embt[:, :, 1])
+                nc.vector.tensor_scalar(out=tab[:, :, 0, 1], in0=embt[:, :, 0], scalar1=-1.0, scalar2=None, op0=MULT)
 
         V, A, G = nc.vector, nc.scalar, nc.gpsimd
-        late = [(n, l) for n in range(10, NP) for l in range(PAIR)]
+        late = [(8, 0)] + [(n, l) for n in range(10, NP) for l in range(PAIR)]
 
         widen(V, 0, 0, 1)
         widen(A, 0, 1, 2)
@@ -272,8 +278,8 @@ def tile_llamaattention_pb_t_w4_kernel(
         xscale(0, 1, 2)
         transposes(2, 0, 2, "vp")
         widen(A, 4, 0, 2)
-        quantise(qx, xq, 0, "x")
         permute_kv_scales()
+        quantise(qx, xq, 0, "x")
         widen(G, 5, 0, 1, "qx0")
         widen(A, 5, 1, 2)
         widen(A, 6, 0, 2)
@@ -281,41 +287,49 @@ def tile_llamaattention_pb_t_w4_kernel(
         kv_matmuls(0, 0)
         kv_matmuls(0, 1)
         kr_matmuls(0)
-        table()
+        table(0)
         quantise(qx, xq, 1, "x")
         widen(G, 7, 0, 1, "qx1")
+        widen(A, 7, 1, 2)
         kv_copy(A, 0, 0)
         kv_copy(A, 0, 1)
-        widen(A, 7, 1, 2)
+        widen(A, 8, 1, 2)
         kv_matmuls(1, 0)
         kv_matmuls(1, 1)
         transposes(3, 0, 2, "xT")
         kv_copy(A, 1, 0)
         kv_copy(A, 1, 1)
-        widen(A, 8, 1, 2)
+        widen(A, 9, 0, 2)
 
         def outputs(n):
             v_matmul(n, 0)
             v_matmul(n, 1)
             kc_matmuls(n)
 
+        def widen_next(eng, tag="xw"):
+            n, l = late[0]
+            late.remove((n, l))
+            widen(eng, n, l, l + 1, tag)
+
         for m in range(2, NP):
             xscale(m, 0, 2)
             if m == 2:
+                table(1)
                 quantise(qk, kq, 0, "kv")
-                widen(G, 8, 0, 1, "qk0")
+                widen_next(G, "qk0")
                 outputs(0)
                 v_copy(A, 0, 0)
                 store_v(0, 0, 1)
-                v_copy(A, 0, 1)
-                store_v(0, 1, 2)
-                kc_copy(A, 0)
             rope_products(m - 2)
             quantise(qx, xq, m, "x")
             quantise(qk, kq, m - 1, "kv")
-            if m - 2 < len(late):
-                widen(G, late[m - 2][0], late[m - 2][1], late[m - 2][1] + 1, "qx%d" % m)
+            if m == 2:
+                v_copy(V, 0, 1)
+                store_v(0, 1, 2)
             rope_sums(G, m - 2)
+            if late:
+                widen_next(G)
+            kc_copy(A, m - 2)
             store_k(m - 2)
             if m < NP - 1:
                 kr_matmuls(m - 1)
@@ -333,9 +347,8 @@ def tile_llamaattention_pb_t_w4_kernel(
             v_copy(A, m - 1, 0)
             v_copy(A, m - 1, 1)
             store_v(m - 1)
-            kc_copy(A, m - 1)
             if m == 2:
-                widen(V, 9, 0, 2)
+                widen_next(A)
         a, b = NP - 2, NP - 1
         kr_matmuls(b)
         outputs(a)

@@ -23,6 +23,7 @@ FLOPS = 2 * B * S * HID * (LAT + H * ROT + H * HD + H * ROT)
 PAIR = 2
 TOK = PAIR * P
 NP = B * R // PAIR
+SUM_FIRST = 3
 
 
 def tile_llamaattention_pb_t_w4_kernel(
@@ -160,8 +161,8 @@ def tile_llamaattention_pb_t_w4_kernel(
 
         def kv_copy(eng, n, l):
             if n not in qk:
-                qk[n] = work.tile([P, TOK, 4], BF16, name="qk", tag="qk0" if n == 0 else "qk",
-                                  bufs=1 if n == 0 else 2, align_bytes=64)
+                qk[n] = work.tile([P, TOK, 4], BF16, name="qk", tag="qk%d" % n if n < SUM_FIRST - 1 else "qk",
+                                  bufs=1 if n < SUM_FIRST - 1 else 2, align_bytes=64)
             copy_on(
                 eng,
                 qk[n][:, l * P : (l + 1) * P, :].rearrange("p (c i) t -> p c t i", i=2),
@@ -180,7 +181,7 @@ def tile_llamaattention_pb_t_w4_kernel(
         def rope_products(n, l0=0, l1=PAIR):
             b, r = where(n)
             if l0 == 0:
-                prod[n] = work.tile([P, PAIR, H, 2, ROT], F32, name="prod", bufs=3)
+                prod[n] = work.tile([P, PAIR, H, 2, ROT], F32, name="prod", bufs=8)
             shape = [P, l1 - l0, H, 2, ROT]
             nc.vector.tensor_tensor(
                 out=prod[n][:, l0:l1],
@@ -320,14 +321,15 @@ def tile_llamaattention_pb_t_w4_kernel(
                 outputs(0)
                 v_copy(A, 0, 0)
                 store_v(0, 0, 1)
+                v_copy(A, 0, 1)
+                store_v(0, 1, 2)
             rope_products(m - 2)
             quantise(qx, xq, m, "x")
             quantise(qk, kq, m - 1, "kv")
-            if m == 2:
-                v_copy(V, 0, 1)
-                store_v(0, 1, 2)
+            if m < SUM_FIRST:
+                widen_next(G, "qk%d" % (m - 1))
             rope_sums(G, m - 2)
-            if late:
+            if m >= SUM_FIRST and late:
                 widen_next(G)
             kc_copy(A, m - 2)
             store_k(m - 2)
@@ -347,7 +349,7 @@ def tile_llamaattention_pb_t_w4_kernel(
             v_copy(A, m - 1, 0)
             v_copy(A, m - 1, 1)
             store_v(m - 1)
-            if m == 2:
+            if m == 6:
                 widen_next(A)
         a, b = NP - 2, NP - 1
         kr_matmuls(b)

@@ -57,7 +57,7 @@ def tile_llamaattention_pb_t_w4_kernel(
         w_r = keep.tile([P, 512], U8, name="w_r", align_bytes=64)
         embt = keep.tile([P, R, 2, HALF], BF16, name="embt")
         tab = keep.tile([P, R, 2, 2, HALF], BF16, name="tab")
-        ident = keep.tile([P, P], F32, name="ident")
+        ident = keep.tile([P, P], BF16, name="ident")
 
         def load_x(i):
             b, r0, r1 = x_cuts[i]
@@ -118,20 +118,19 @@ def tile_llamaattention_pb_t_w4_kernel(
             copy_on(eng, wide[:], src)
 
         def transposes(n, l0, l1, tag):
-            bank = psum.tile([P, 2, l1 - l0, P], F32, name="xT", tag=tag, bufs=2 if tag in ("xT", "kvp", "vp") else 1)
+            bank = psum.tile([P, l1 - l0, 4, P], BF16, name="xT", tag=tag, bufs=2 if tag in ("xT", "kvp", "vp") else 1)
             xT[n, l0] = bank
             for l in range(l0, l1):
-                words = xw[n, l].bitcast(F32)
-                for u in range(2):
-                    nc.tensor.transpose(bank[:, u, l - l0, :], words[:, u : 256 : 2], ident[:])
+                for t in range(4):
+                    nc.tensor.matmul(bank[:, l - l0, t, :], lhsT=xw[n, l][:, t : HID : 4], rhs=ident[:], start=True, stop=True)
 
         def xscale(n, l0, l1):
             if n not in qx:
                 qx[n] = work.tile([P, TOK, 4], BF16, name="qx", tag="qx%d" % n, bufs=1, align_bytes=64)
             nc.vector.tensor_tensor(
-                out=qx[n][:, l0 * P : l1 * P].rearrange("p n (u e) -> p n u e", u=2),
-                in0=xT[n, l0][:].bitcast(BF16).rearrange("p u l (n e) -> p (l n) u e", e=2),
-                in1=xsc[:].rearrange("p (u e) -> p u e", u=2).unsqueeze(1).broadcast_to([P, (l1 - l0) * P, 2, 2]),
+                out=qx[n][:, l0 * P : l1 * P].rearrange("p (l n) t -> p l n t", n=P),
+                in0=xT[n, l0][:].rearrange("p l t n -> p l n t"),
+                in1=xsc[:].unsqueeze(1).unsqueeze(1).broadcast_to([P, l1 - l0, P, 4]),
                 op=MULT,
             )
 

@@ -12,6 +12,7 @@ FP8 = mybir.dt.float8_e4m3fn
 FP8X4 = mybir.dt.float8_e4m3fn_x4
 FP4X4 = mybir.dt.float4_e2m1fn_x4
 ADD = mybir.AluOpType.add
+SUB = mybir.AluOpType.subtract
 MULT = mybir.AluOpType.mult
 
 B, S, H, HD, HID, LAT = 2, 2048, 4, 128, 512, 512
@@ -23,7 +24,7 @@ FLOPS = 2 * B * S * HID * (LAT + H * ROT + H * HD + H * ROT)
 PAIR = 2
 TOK = PAIR * P
 NP = B * R // PAIR
-SUM_FIRST = 3
+LONG = 640
 
 
 def tile_llamaattention_pb_t_w4_kernel(
@@ -55,8 +56,11 @@ def tile_llamaattention_pb_t_w4_kernel(
         w_v = keep.tile([P, 1024], U8, name="w_v", align_bytes=64)
         w_k = keep.tile([P, 512], U8, name="w_k", align_bytes=64)
         w_r = keep.tile([P, 512], U8, name="w_r", align_bytes=64)
+        w_r3 = keep.tile([P, 512], U8, name="w_r3", align_bytes=64)
+        s_r3 = keep.tile([P, 256], U8, name="s_r3", align_bytes=64)
         embt = keep.tile([P, R, 2, HALF], BF16, name="embt")
-        tab = keep.tile([P, R, 2, 2, HALF], BF16, name="tab")
+        tab4 = keep.tile([P, R // 4, PAIR, 2, 2, HALF], BF16, name="tab4")
+        tab3 = keep.tile([P, R // 4, PAIR, 3, HALF], F32, name="tab3")
         ident = keep.tile([P, P], BF16, name="ident")
 
         def load_x(i):
@@ -99,6 +103,8 @@ def tile_llamaattention_pb_t_w4_kernel(
 
         xw, xT, qx, qk, xq, kq, kvp, krp, kt, vt, vp, kcp, prod = ({}, {}, {}, {}, {}, {}, {}, {}, {}, {}, {}, {}, {})
 
+        parts = {}
+
         def where(n):
             return n // (R // PAIR), PAIR * (n % (R // PAIR))
 
@@ -118,7 +124,7 @@ def tile_llamaattention_pb_t_w4_kernel(
             copy_on(eng, wide[:], src)
 
         def transposes(n, l0, l1, tag):
-            bank = psum.tile([P, l1 - l0, 4, P], BF16, name="xT", tag=tag, bufs=2 if tag in ("xT", "kvp", "vp") else 1)
+            bank = psum.tile([P, l1 - l0, 4, P], BF16, name="xT", tag=tag, bufs=2 if tag == "vp" else 1)
             xT[n, l0] = bank
             for l in range(l0, l1):
                 for t in range(4):
@@ -160,34 +166,57 @@ def tile_llamaattention_pb_t_w4_kernel(
 
         def kv_copy(eng, n, l):
             if n not in qk:
-                qk[n] = work.tile([P, TOK, 4], BF16, name="qk", tag="qk%d" % n if n < SUM_FIRST - 1 else "qk",
-                                  bufs=1 if n < SUM_FIRST - 1 else 2, align_bytes=64)
+                qk[n] = work.tile([P, TOK, 4], BF16, name="qk", tag="qk0" if n == 0 else "qk",
+                                  bufs=1 if n == 0 else 2, align_bytes=64)
             copy_on(
                 eng,
                 qk[n][:, l * P : (l + 1) * P, :].rearrange("p (c i) t -> p c t i", i=2),
                 kvp[n, l][:].rearrange("p t (c i) -> p c t i", i=2),
             )
 
-        def kr_matmuls(n, tag="krp"):
-            krp[n] = psum.tile([P, PAIR, H * ROT], F32, name="krp", tag=tag, bufs=1 if tag == "krp" else 2)
-            for l in range(PAIR):
+        def kr_matmuls(n, l0=0, l1=PAIR, tag="krp"):
+            for l in range(l0, l1):
                 codes, scales = operand(xq[n], l)
-                nc.tensor.matmul_mx(
-                    krp[n][:, l], lhsT=codes, lhsT_scale=scales,
-                    rhs=w_r[:].bitcast(FP4X4), rhs_scale=s_r[:], start=True, stop=True,
-                )
+                if n % 2 == 0:
+                    if l == 0:
+                        krp[n] = psum.tile([P, PAIR, H * ROT], F32, name="krp", tag=tag, bufs=2 if tag == "krp" else 1)
+                    passes = ((krp[n][:, l], w_r, s_r, 0, 256, True, True),)
+                else:
+                    krp[n, l] = psum.tile([P, 3, H * HALF], F32, name="krp", tag="krp", bufs=2)
+                    passes = (
+                        (krp[n, l][:, 0:2].rearrange("p c m -> p (c m)"), w_r3, s_r3, 0, 256, True, True),
+                        (krp[n, l][:, 2], w_r3, s_r3, 0, 128, True, False),
+                        (krp[n, l][:, 2], w_r3, s_r3, 128, 256, False, True),
+                    )
+                for out, w, s, lo, hi, start, stop in passes:
+                    nc.tensor.matmul_mx(
+                        out, lhsT=codes, lhsT_scale=scales,
+                        rhs=w[:, 2 * lo : 2 * hi].bitcast(FP4X4), rhs_scale=s[:, lo:hi],
+                        start=start, stop=stop,
+                    )
 
         def rope_products(n, l0=0, l1=PAIR):
             b, r = where(n)
-            if l0 == 0:
-                prod[n] = work.tile([P, PAIR, H, 2, ROT], F32, name="prod", bufs=8)
-            shape = [P, l1 - l0, H, 2, ROT]
-            nc.vector.tensor_tensor(
-                out=prod[n][:, l0:l1],
-                in0=krp[n][:, l0:l1].rearrange("p l (h d) -> p l h d", h=H).unsqueeze(3).broadcast_to(shape),
-                in1=tab[:, r + l0 : r + l1].rearrange("p l a c j -> p l a (c j)").unsqueeze(2).broadcast_to(shape),
-                op=MULT,
-            )
+            if n % 2 == 0:
+                if l0 == 0:
+                    prod[n] = work.tile([P, PAIR, H, 2, ROT], F32, name="prod", tag="prod", bufs=8)
+                shape = [P, l1 - l0, H, 2, ROT]
+                nc.vector.tensor_tensor(
+                    out=prod[n][:, l0:l1],
+                    in0=krp[n][:, l0:l1].rearrange("p l (h d) -> p l h d", h=H).unsqueeze(3).broadcast_to(shape),
+                    in1=tab4[:, r // 4, l0:l1].rearrange("p l a c j -> p l a (c j)").unsqueeze(2).broadcast_to(shape),
+                    op=MULT,
+                )
+                return
+            for l in range(l0, l1):
+                if l == 0:
+                    prod[n] = work.tile([P, PAIR, H, 3, HALF], F32, name="prod", tag="prod", bufs=8)
+                nc.vector.tensor_tensor(
+                    out=prod[n][:, l].rearrange("p h c j -> p c h j"),
+                    in0=krp[n, l][:].rearrange("p c (h j) -> p c h j", h=H),
+                    in1=tab3[:, r // 4, l].unsqueeze(2).broadcast_to([P, 3, H, HALF]),
+                    op=MULT,
+                )
 
         def k_tile(n):
             if n not in kt:
@@ -198,11 +227,14 @@ def tile_llamaattention_pb_t_w4_kernel(
             return kt[n]
 
         def rope_sums(eng, n, l0=0, l1=PAIR):
-            m = prod[n][:, l0:l1].rearrange("p l h a (c j) -> p (l h) a c j", c=2)
-            eng.tensor_tensor(
-                out=k_tile(n)[:, l0:l1].rearrange("p l h (a j) -> p (l h) a j", j=HALF)[:, :, 2:4, :],
-                in0=m[:, :, :, 0, :], in1=m[:, :, :, 1, :], op=ADD,
-            )
+            out = k_tile(n)[:, l0:l1].rearrange("p l h (a j) -> p (l h) a j", j=HALF)[:, :, 2:4, :]
+            if n % 2 == 0:
+                m = prod[n][:, l0:l1].rearrange("p l h a (c j) -> p (l h) a c j", c=2)
+                eng.tensor_tensor(out=out, in0=m[:, :, :, 0, :], in1=m[:, :, :, 1, :], op=ADD)
+            else:
+                m = prod[n][:, l0:l1].rearrange("p l h c j -> p (l h) c j")
+                eng.tensor_tensor(
+                    out=out, in0=m[:, :, 2:3, :].broadcast_to([P, (l1 - l0) * H, 2, HALF]), in1=m[:, :, 0:2, :], op=SUB)
 
         def v_matmul(n, l):
             codes, scales = operand(kq[n], l)
@@ -254,15 +286,40 @@ def tile_llamaattention_pb_t_w4_kernel(
                 out=s_kv[:].rearrange("p (t m) -> p t m", t=4),
                 in_=s_kv_raw[:].rearrange("p (m t) -> p t m", t=4))
 
-        def table(a):
+        rows = embt[:].rearrange("p (g o l) w j -> p g o l w j", o=2, l=PAIR)
+
+        def table4(a):
+            even = rows[:, :, 0]
             if a == 1:
-                nc.vector.tensor_copy(out=tab[:, :, 1], in_=embt[:])
+                nc.vector.tensor_copy(out=tab4[:, :, :, 1], in_=even)
             else:
-                nc.vector.tensor_copy(out=tab[:, :, 0, 0], in_=embt[:, :, 1])
-                nc.vector.tensor_scalar(out=tab[:, :, 0, 1], in0=embt[:, :, 0], scalar1=-1.0, scalar2=None, op0=MULT)
+                nc.vector.tensor_copy(out=tab4[:, :, :, 0, 0], in_=even[:, :, :, 1])
+                nc.vector.tensor_scalar(out=tab4[:, :, :, 0, 1], in0=even[:, :, :, 0], scalar1=-1.0, scalar2=None, op0=MULT)
+
+        def table3():
+            sin, cos = rows[:, :, 1, :, 0], rows[:, :, 1, :, 1]
+            nc.vector.tensor_tensor(out=tab3[:, :, :, 0], in0=cos, in1=sin, op=ADD)
+            nc.vector.tensor_tensor(out=tab3[:, :, :, 1], in0=cos, in1=sin, op=SUB)
+            nc.vector.tensor_copy(out=tab3[:, :, :, 2], in_=cos)
+
+        def permute_r():
+            for dst, src in ((w_r3, w_r), (s_r3, s_r)):
+                for a in range(2):
+                    nc.scalar.copy(
+                        out=dst[:].bitcast(U32).rearrange("p (a h c) -> p a h c", a=2, h=H)[:, 1 - a],
+                        in_=src[:].bitcast(U32).rearrange("p (h a c) -> p a h c", a=2, h=H)[:, a])
+
+        def widen_part(eng, n, c0, c1):
+            b, r = where(n)
+            r0 = max(c[1] for c in x_cuts if c[0] == b and c[1] <= r)
+            if c0 == 0:
+                parts[n] = work.tile([P, PAIR * HID], BF16, name="xw", tag="xw", bufs=16, align_bytes=64)
+                for l in range(PAIR):
+                    xw[n, l] = parts[n][:, l * HID : (l + 1) * HID]
+            src = xb[b, r0][:, (r - r0) * HID + c0 : (r - r0) * HID + c1].bitcast(FP8)
+            copy_on(eng, parts[n][:, c0:c1], src)
 
         V, A, G = nc.vector, nc.scalar, nc.gpsimd
-        late = [(8, 0)] + [(n, l) for n in range(10, NP) for l in range(PAIR)]
 
         widen(V, 0, 0, 1)
         widen(A, 0, 1, 2)
@@ -270,7 +327,7 @@ def tile_llamaattention_pb_t_w4_kernel(
         transposes(0, 1, 2, "xT")
         widen(A, 1, 0, 2)
         permute_kv_words()
-        transposes(1, 0, 2, "xT")
+        transposes(1, 0, 2, "vp")
         widen(A, 2, 0, 2)
         widen(G, 3, 0, 1)
         widen(A, 3, 1, 2)
@@ -287,13 +344,15 @@ def tile_llamaattention_pb_t_w4_kernel(
         kv_matmuls(0, 0)
         kv_matmuls(0, 1)
         kr_matmuls(0)
-        table(0)
+        table4(0)
+        table4(1)
         quantise(qx, xq, 1, "x")
         widen(G, 7, 0, 1, "qx1")
         widen(A, 7, 1, 2)
         kv_copy(A, 0, 0)
         kv_copy(A, 0, 1)
         widen(A, 8, 1, 2)
+        permute_r()
         kv_matmuls(1, 0)
         kv_matmuls(1, 1)
         transposes(3, 0, 2, "xT")
@@ -306,18 +365,13 @@ def tile_llamaattention_pb_t_w4_kernel(
             v_matmul(n, 1)
             kc_matmuls(n)
 
-        def widen_next(eng, tag="xw"):
-            n, l = late[0]
-            late.remove((n, l))
-            widen(eng, n, l, l + 1, tag)
-
         for m in range(2, NP):
             xscale(m, 0, 2)
             if m == 2:
-                table(1)
                 quantise(qk, kq, 0, "kv")
-                widen_next(G, "qk0")
+                widen(G, 8, 0, 1, "qk0")
                 outputs(0)
+                kr_matmuls(1, 0, 1)
                 v_copy(A, 0, 0)
                 store_v(0, 0, 1)
                 v_copy(A, 0, 1)
@@ -325,15 +379,20 @@ def tile_llamaattention_pb_t_w4_kernel(
             rope_products(m - 2)
             quantise(qx, xq, m, "x")
             quantise(qk, kq, m - 1, "kv")
-            if m < SUM_FIRST:
-                widen_next(G, "qk%d" % (m - 1))
+            if m == 2:
+                table3()
             rope_sums(G, m - 2)
-            if m >= SUM_FIRST and late:
-                widen_next(G)
+            if m == 2:
+                widen_part(G, 10, 0, PAIR * HID - LONG)
+            elif m < NP - 3:
+                if m % 2:
+                    widen_part(G, 11 + (m - 3) // 2, 0, LONG)
+                else:
+                    widen_part(G, 11 + (m - 3) // 2, LONG, PAIR * HID)
             kc_copy(A, m - 2)
             store_k(m - 2)
             if m < NP - 1:
-                kr_matmuls(m - 1)
+                kr_matmuls(m - 1, (m - 1) % 2, PAIR)
             kv_matmuls(m, 0)
             kv_matmuls(m, 1)
             if m == NP - 1:
@@ -343,16 +402,20 @@ def tile_llamaattention_pb_t_w4_kernel(
             outputs(m - 1)
             if m + 2 < NP:
                 transposes(m + 2, 0, 2, "xT")
+            if m % 2:
+                kr_matmuls(m, 0, 1)
             if m == NP - 2:
-                kr_matmuls(m, "xT")
+                kr_matmuls(m, 0, 2, "xT")
             v_copy(A, m - 1, 0)
             v_copy(A, m - 1, 1)
             store_v(m - 1)
-            if m == 6:
-                widen_next(A)
+            if m == 2:
+                widen_part(A, 10, PAIR * HID - LONG, PAIR * HID)
         a, b = NP - 2, NP - 1
+        v_matmul(a, 0)
+        v_matmul(a, 1)
         kr_matmuls(b)
-        outputs(a)
+        kc_matmuls(a)
         rope_products(a, 0, 1)
         kv_copy(V, b, 0)
         kv_copy(A, b, 1)

@@ -7,6 +7,7 @@ F32 = mybir.dt.float32
 BF16 = mybir.dt.bfloat16
 I32 = mybir.dt.int32
 U32 = mybir.dt.uint32
+U16 = mybir.dt.uint16
 U8 = mybir.dt.uint8
 FP8 = mybir.dt.float8_e4m3fn
 FP8X4 = mybir.dt.float8_e4m3fn_x4
@@ -45,7 +46,7 @@ def tile_llamaattention_pb_t_w4_kernel(
         for plane in (s_kv_raw, s_r, s_v, s_k):
             nc.vector.memset(plane[:].bitcast(I32), 0)
 
-        x_cuts = ((0, 0, 2), (0, 2, 4), (0, 4, 8), (0, 8, 12), (0, 12, 16), (1, 0, 4), (1, 4, 12), (1, 12, 16))
+        x_cuts = ((0, 0, 1), (0, 1, 4), (0, 4, 8), (0, 8, 12), (0, 12, 16), (1, 0, 4), (1, 4, 12), (1, 12, 16))
         xb = {}
         for b, r0, r1 in x_cuts:
             xb[b, r0] = keep.tile([P, (r1 - r0) * HID], U8, name="xb%d_%d" % (b, r0))
@@ -84,8 +85,8 @@ def tile_llamaattention_pb_t_w4_kernel(
         load_words(w_kv_raw, wkv_words)
         nc.sync.dma_start(out=xsc[:], in_=x_scale.rearrange("a b (p t) -> p (a b t)", t=4))
         load_x(2)
-        load_scales(s_kv_raw, wkv_scales)
         load_x(3)
+        load_scales(s_kv_raw, wkv_scales)
         load_x(4)
         nc.sync.dma_start(
             out=embt[:].rearrange("p r w j -> p r (w j)"),
@@ -116,7 +117,7 @@ def tile_llamaattention_pb_t_w4_kernel(
 
         def widen(eng, n, l0, l1, tag="xw"):
             b, r = where(n)
-            r0 = max(c[1] for c in x_cuts if c[0] == b and c[1] <= r)
+            r0 = max(c[1] for c in x_cuts if c[0] == b and c[1] <= r + l0)
             wide = work.tile([P, (l1 - l0) * HID], BF16, name="xw", tag=tag, bufs=16 if tag == "xw" else 1, align_bytes=64)
             for l in range(l0, l1):
                 xw[n, l] = wide[:, (l - l0) * HID : (l - l0 + 1) * HID]
@@ -277,9 +278,9 @@ def tile_llamaattention_pb_t_w4_kernel(
             store(k_out, kt[n][:].rearrange("p l h d -> p l (h d)"), n, l0, l1)
 
         def permute_kv_words():
-            nc.vector.tensor_copy(
-                out=w_kv[:].rearrange("p (t m c) -> p t m c", t=4, c=2),
-                in_=w_kv_raw[:].rearrange("p (m t c) -> p t m c", t=4, c=2))
+            nc.scalar.copy(
+                out=w_kv[:].bitcast(U16).rearrange("p (t m) -> p t m", t=4),
+                in_=w_kv_raw[:].bitcast(U16).rearrange("p (m t) -> p t m", t=4))
 
         def permute_kv_scales():
             nc.vector.tensor_copy(
@@ -300,7 +301,6 @@ def tile_llamaattention_pb_t_w4_kernel(
             sin, cos = rows[:, :, 1, :, 0], rows[:, :, 1, :, 1]
             nc.vector.tensor_tensor(out=tab3[:, :, :, 0], in0=cos, in1=sin, op=ADD)
             nc.vector.tensor_tensor(out=tab3[:, :, :, 1], in0=cos, in1=sin, op=SUB)
-            nc.vector.tensor_copy(out=tab3[:, :, :, 2], in_=cos)
 
         def permute_r():
             for dst, src in ((w_r3, w_r), (s_r3, s_r)):
@@ -322,10 +322,10 @@ def tile_llamaattention_pb_t_w4_kernel(
         V, A, G = nc.vector, nc.scalar, nc.gpsimd
 
         widen(V, 0, 0, 1)
-        widen(A, 0, 1, 2)
+        widen(V, 0, 1, 2)
         transposes(0, 0, 1, "kcp")
         transposes(0, 1, 2, "xT")
-        widen(A, 1, 0, 2)
+        widen(V, 1, 0, 2)
         permute_kv_words()
         transposes(1, 0, 2, "vp")
         widen(A, 2, 0, 2)
@@ -337,8 +337,8 @@ def tile_llamaattention_pb_t_w4_kernel(
         widen(A, 4, 0, 2)
         permute_kv_scales()
         quantise(qx, xq, 0, "x")
-        widen(G, 5, 0, 1, "qx0")
-        widen(A, 5, 1, 2)
+        widen(G, 7, 0, 1, "qx0")
+        widen(A, 5, 0, 2)
         widen(A, 6, 0, 2)
         xscale(1, 0, 2)
         kv_matmuls(0, 0)
@@ -347,12 +347,12 @@ def tile_llamaattention_pb_t_w4_kernel(
         table4(0)
         table4(1)
         quantise(qx, xq, 1, "x")
-        widen(G, 7, 0, 1, "qx1")
+        widen(G, 8, 1, 2, "qx1")
         widen(A, 7, 1, 2)
         kv_copy(A, 0, 0)
         kv_copy(A, 0, 1)
-        widen(A, 8, 1, 2)
         permute_r()
+        nc.scalar.copy(out=tab3[:, :, :, 2], in_=rows[:, :, 1, :, 1])
         kv_matmuls(1, 0)
         kv_matmuls(1, 1)
         transposes(3, 0, 2, "xT")

@@ -25,7 +25,8 @@ FLOPS = 2 * B * S * HID * (LAT + H * ROT + H * HD + H * ROT)
 PAIR = 2
 TOK = PAIR * P
 NP = B * R // PAIR
-LONG = 640
+LONG, SHORT = 672, 480
+LATE = 10
 
 
 def tile_llamaattention_pb_t_w4_kernel(
@@ -46,11 +47,13 @@ def tile_llamaattention_pb_t_w4_kernel(
         for plane in (s_kv_raw, s_r, s_v, s_k):
             nc.vector.memset(plane[:].bitcast(I32), 0)
 
-        x_cuts = ((0, 0, 1), (0, 1, 4), (0, 4, 8), (0, 8, 12), (0, 12, 16), (1, 0, 4), (1, 4, 12), (1, 12, 16))
+        x_cuts = ((0, 0, 1), (0, 1, 4), (0, 4, 8), (0, 8, 12), (0, 12, 16), (1, 0, 4))
         xb = {}
         for b, r0, r1 in x_cuts:
             xb[b, r0] = keep.tile([P, (r1 - r0) * HID], U8, name="xb%d_%d" % (b, r0))
         xsc = keep.tile([P, 4], F32, name="xsc")
+        late_bytes = keep.tile([P, (NP - LATE) * PAIR * HID], U8, name="late_bytes")
+        late_wide = keep.tile([P, (NP - LATE) * PAIR * HID], BF16, name="late_wide", align_bytes=64)
         w_kv_raw = keep.tile([P, 1024], U8, name="w_kv_raw", align_bytes=64)
         w_kv = keep.tile([P, 1024], U8, name="w_kv", align_bytes=64)
         s_kv = keep.tile([P, 512], U8, name="s_kv", align_bytes=64)
@@ -99,12 +102,11 @@ def tile_llamaattention_pb_t_w4_kernel(
         load_scales(s_v, wv_scales)
         load_words(w_k, wk_words)
         load_scales(s_k, wk_scales)
-        load_x(6)
-        load_x(7)
+        late_rows = x_bytes[1].rearrange("(p r) k -> p (r k)", p=P)[:, 4 * HID :]
+        for c0, c1 in ((0, 4096), (4096, 6144)):
+            nc.sync.dma_start(out=late_bytes[:, c0:c1], in_=late_rows[:, c0:c1])
 
         xw, xT, qx, qk, xq, kq, kvp, krp, kt, vt, vp, kcp, prod = ({}, {}, {}, {}, {}, {}, {}, {}, {}, {}, {}, {}, {})
-
-        parts = {}
 
         def where(n):
             return n // (R // PAIR), PAIR * (n % (R // PAIR))
@@ -118,7 +120,7 @@ def tile_llamaattention_pb_t_w4_kernel(
         def widen(eng, n, l0, l1, tag="xw"):
             b, r = where(n)
             r0 = max(c[1] for c in x_cuts if c[0] == b and c[1] <= r + l0)
-            wide = work.tile([P, (l1 - l0) * HID], BF16, name="xw", tag=tag, bufs=16 if tag == "xw" else 1, align_bytes=64)
+            wide = work.tile([P, (l1 - l0) * HID], BF16, name="xw", tag=tag, bufs=10 if tag == "xw" else 1, align_bytes=64)
             for l in range(l0, l1):
                 xw[n, l] = wide[:, (l - l0) * HID : (l - l0 + 1) * HID]
             src = xb[b, r0][:, (r - r0 + l0) * HID : (r - r0 + l1) * HID].bitcast(FP8)
@@ -309,15 +311,15 @@ def tile_llamaattention_pb_t_w4_kernel(
                         out=dst[:].bitcast(U32).rearrange("p (a h c) -> p a h c", a=2, h=H)[:, 1 - a],
                         in_=src[:].bitcast(U32).rearrange("p (h a c) -> p a h c", a=2, h=H)[:, a])
 
-        def widen_part(eng, n, c0, c1):
-            b, r = where(n)
-            r0 = max(c[1] for c in x_cuts if c[0] == b and c[1] <= r)
-            if c0 == 0:
-                parts[n] = work.tile([P, PAIR * HID], BF16, name="xw", tag="xw", bufs=16, align_bytes=64)
-                for l in range(PAIR):
-                    xw[n, l] = parts[n][:, l * HID : (l + 1) * HID]
-            src = xb[b, r0][:, (r - r0) * HID + c0 : (r - r0) * HID + c1].bitcast(FP8)
-            copy_on(eng, parts[n][:, c0:c1], src)
+        for n in range(LATE, NP):
+            for l in range(PAIR):
+                c = ((n - LATE) * PAIR + l) * HID
+                xw[n, l] = late_wide[:, c : c + HID]
+
+        def widen_late(m):
+            c0 = (m - 2) // 2 * (LONG + SHORT) + m % 2 * SHORT
+            c1 = min(c0 + (LONG if m % 2 else SHORT), (NP - LATE) * PAIR * HID)
+            nc.gpsimd.tensor_copy(out=late_wide[:, c0:c1], in_=late_bytes[:, c0:c1].bitcast(FP8))
 
         V, A, G = nc.vector, nc.scalar, nc.gpsimd
 
@@ -382,13 +384,8 @@ def tile_llamaattention_pb_t_w4_kernel(
             if m == 2:
                 table3()
             rope_sums(G, m - 2)
-            if m == 2:
-                widen_part(G, 10, 0, PAIR * HID - LONG)
-            elif m < NP - 3:
-                if m % 2:
-                    widen_part(G, 11 + (m - 3) // 2, 0, LONG)
-                else:
-                    widen_part(G, 11 + (m - 3) // 2, LONG, PAIR * HID)
+            if m < NP - 3:
+                widen_late(m)
             kc_copy(A, m - 2)
             store_k(m - 2)
             if m < NP - 1:
@@ -409,8 +406,6 @@ def tile_llamaattention_pb_t_w4_kernel(
             v_copy(A, m - 1, 0)
             v_copy(A, m - 1, 1)
             store_v(m - 1)
-            if m == 2:
-                widen_part(A, 10, PAIR * HID - LONG, PAIR * HID)
         a, b = NP - 2, NP - 1
         v_matmul(a, 0)
         v_matmul(a, 1)

@@ -391,9 +391,9 @@ def tile_llamaattention_pb_t_w4_kernel(
             if m < NP - 1:
                 kr_matmuls(m - 1, (m - 1) % 2, PAIR)
             kv_matmuls(m, 0)
-            kv_matmuls(m, 1)
             if m == NP - 1:
                 break
+            kv_matmuls(m, 1)
             kv_copy(A, m, 0)
             kv_copy(A, m, 1)
             outputs(m - 1)
@@ -408,21 +408,23 @@ def tile_llamaattention_pb_t_w4_kernel(
             store_v(m - 1)
         a, b = NP - 2, NP - 1
         v_matmul(a, 0)
+        kv_matmuls(b, 1)
         v_matmul(a, 1)
-        kr_matmuls(b)
         kc_matmuls(a)
+        kr_matmuls(b)
         rope_products(a, 0, 1)
+        rope_sums(G, a, 0, 1)
         kv_copy(V, b, 0)
-        kv_copy(A, b, 1)
-        rope_products(a, 1, 2)
-        quantise(qk, kq, b, "kv")
-        rope_sums(G, a)
-        rope_products(b)
         v_copy(A, a, 0)
+        kv_copy(V, b, 1)
         v_copy(A, a, 1)
         store_v(a)
+        rope_products(a, 1, 2)
+        quantise(qk, kq, b, "kv")
+        rope_sums(G, a, 1, 2)
         kc_copy(A, a)
         store_k(a)
+        rope_products(b)
         rope_sums(G, b)
         outputs(b)
         v_copy(A, b, 0)

from contextlib import ExitStack

import concourse.mybir as mybir
from concourse.masks import make_identity

F32 = mybir.dt.float32
BF16 = mybir.dt.bfloat16
I32 = mybir.dt.int32
U32 = mybir.dt.uint32
U16 = mybir.dt.uint16
U8 = mybir.dt.uint8
FP8 = mybir.dt.float8_e4m3fn
FP8X4 = mybir.dt.float8_e4m3fn_x4
FP4X4 = mybir.dt.float4_e2m1fn_x4
ADD = mybir.AluOpType.add
SUB = mybir.AluOpType.subtract
MULT = mybir.AluOpType.mult

B, S, H, HD, HID, LAT = 2, 2048, 4, 128, 512, 512
ROT, HALF = 64, 32
P = 128
R = S // P
FLOPS = 2 * B * S * HID * (LAT + H * ROT + H * HD + H * ROT)

PAIR = 2
TOK = PAIR * P
NP = B * R // PAIR
LONG, SHORT = 672, 480
LATE = 10


def tile_llamaattention_pb_t_w4_kernel(
    tc, x_bytes, x_scale, emb, wkv_words, wkv_scales, wk_words, wk_scales,
    wv_words, wv_scales, wr_words, wr_scales, k_out, v_out,
):
    nc = tc.nc
    with ExitStack() as ctx:
        keep = ctx.enter_context(tc.tile_pool(name="keep", bufs=1))
        work = ctx.enter_context(tc.tile_pool(name="work", bufs=3))
        psum = ctx.enter_context(tc.psum_pool(name="psum", bufs=1))
        ctx.enter_context(tc.manual_schedule())

        s_kv_raw = keep.tile([P, 512], U8, name="s_kv_raw", align_bytes=64)
        s_r = keep.tile([P, 256], U8, name="s_r", align_bytes=64)
        s_v = keep.tile([P, 512], U8, name="s_v", align_bytes=64)
        s_k = keep.tile([P, 256], U8, name="s_k", align_bytes=64)
        for plane in (s_kv_raw, s_r, s_v, s_k):
            nc.vector.memset(plane[:].bitcast(I32), 0)

        x_cuts = ((0, 0, 1), (0, 1, 4), (0, 4, 8), (0, 8, 12), (0, 12, 16), (1, 0, 4))
        xb = {}
        for b, r0, r1 in x_cuts:
            xb[b, r0] = keep.tile([P, (r1 - r0) * HID], U8, name="xb%d_%d" % (b, r0))
        xsc = keep.tile([P, 4], F32, name="xsc")
        late_bytes = keep.tile([P, (NP - LATE) * PAIR * HID], U8, name="late_bytes")
        late_wide = keep.tile([P, (NP - LATE) * PAIR * HID], BF16, name="late_wide", align_bytes=64)
        w_kv_raw = keep.tile([P, 1024], U8, name="w_kv_raw", align_bytes=64)
        w_kv = keep.tile([P, 1024], U8, name="w_kv", align_bytes=64)
        s_kv = keep.tile([P, 512], U8, name="s_kv", align_bytes=64)
        w_v = keep.tile([P, 1024], U8, name="w_v", align_bytes=64)
        w_k = keep.tile([P, 512], U8, name="w_k", align_bytes=64)
        w_r = keep.tile([P, 512], U8, name="w_r", align_bytes=64)
        w_r3 = keep.tile([P, 512], U8, name="w_r3", align_bytes=64)
        s_r3 = keep.tile([P, 256], U8, name="s_r3", align_bytes=64)
        embt = keep.tile([P, R, 2, HALF], BF16, name="embt")
        tab4 = keep.tile([P, R // 4, PAIR, 2, 2, HALF], BF16, name="tab4")
        tab3 = keep.tile([P, R // 4, PAIR, 3, HALF], F32, name="tab3")
        ident = keep.tile([P, P], BF16, name="ident")

        def load_x(i):
            b, r0, r1 = x_cuts[i]
            rows = x_bytes[b].rearrange("(p r) k -> p r k", p=P)[:, r0:r1, :]
            nc.sync.dma_start(out=xb[b, r0][:].rearrange("p (r k) -> p r k", k=HID), in_=rows)

        def load_words(tile, src):
            nc.sync.dma_start(out=tile[:].bitcast(I32), in_=src[0].bitcast(I32))

        def load_scales(plane, src):
            for q in range(4):
                nc.sync.dma_start(
                    out=plane[32 * q : 32 * q + 4, :].bitcast(I32),
                    in_=src[0, 4 * q : 4 * q + 4, :].bitcast(I32),
                )

        make_identity(nc, ident[:])
        load_x(0)
        load_x(1)
        load_words(w_kv_raw, wkv_words)
        nc.sync.dma_start(out=xsc[:], in_=x_scale.rearrange("a b (p t) -> p (a b t)", t=4))
        load_x(2)
        load_x(3)
        load_scales(s_kv_raw, wkv_scales)
        load_x(4)
        nc.sync.dma_start(
            out=embt[:].rearrange("p r w j -> p r (w j)"),
            in_=emb[0, 0].rearrange("(p r) c -> p r c", p=P),
        )
        load_words(w_r, wr_words)
        load_scales(s_r, wr_scales)
        load_x(5)
        load_words(w_v, wv_words)
        load_scales(s_v, wv_scales)
        load_words(w_k, wk_words)
        load_scales(s_k, wk_scales)
        late_rows = x_bytes[1].rearrange("(p r) k -> p (r k)", p=P)[:, 4 * HID :]
        for c0, c1 in ((0, 4096), (4096, 6144)):
            nc.sync.dma_start(out=late_bytes[:, c0:c1], in_=late_rows[:, c0:c1])

        xw, xT, qx, qk, xq, kq, kvp, krp, kt, vt, vp, kcp, prod = ({}, {}, {}, {}, {}, {}, {}, {}, {}, {}, {}, {}, {})

        def where(n):
            return n // (R // PAIR), PAIR * (n % (R // PAIR))

        def copy_on(eng, out, in_):
            if eng is nc.scalar:
                nc.scalar.copy(out=out, in_=in_)
            else:
                eng.tensor_copy(out=out, in_=in_)

        def widen(eng, n, l0, l1, tag="xw"):
            b, r = where(n)
            r0 = max(c[1] for c in x_cuts if c[0] == b and c[1] <= r + l0)
            wide = work.tile([P, (l1 - l0) * HID], BF16, name="xw", tag=tag, bufs=10 if tag == "xw" else 1, align_bytes=64)
            for l in range(l0, l1):
                xw[n, l] = wide[:, (l - l0) * HID : (l - l0 + 1) * HID]
            src = xb[b, r0][:, (r - r0 + l0) * HID : (r - r0 + l1) * HID].bitcast(FP8)
            copy_on(eng, wide[:], src)

        def transposes(n, l0, l1, tag):
            bank = psum.tile([P, l1 - l0, 4, P], BF16, name="xT", tag=tag, bufs=2 if tag == "vp" else 1)
            xT[n, l0] = bank
            for l in range(l0, l1):
                for t in range(4):
                    nc.tensor.matmul(bank[:, l - l0, t, :], lhsT=xw[n, l][:, t : HID : 4], rhs=ident[:], start=True, stop=True)

        def xscale(n, l0, l1):
            if n not in qx:
                qx[n] = work.tile([P, TOK, 4], BF16, name="qx", tag="qx%d" % n, bufs=1, align_bytes=64)
            nc.vector.tensor_tensor(
                out=qx[n][:, l0 * P : l1 * P].rearrange("p (l n) t -> p l n t", n=P),
                in0=xT[n, l0][:].rearrange("p l t n -> p l n t"),
                in1=xsc[:].unsqueeze(1).unsqueeze(1).broadcast_to([P, l1 - l0, P, 4]),
                op=MULT,
            )

        def quantise(src, dst, n, name):
            codes = work.tile([P, TOK], U32, name=name + "_codes", bufs=3, align_bytes=64)
            scales = work.tile([P, TOK], U8, name=name + "_scales", bufs=3, align_bytes=64)
            dst[n] = (codes, scales)
            nc.vector.quantize_mx(
                out=codes[:].bitcast(FP8X4), scales=scales[:], in_=src[n][:].rearrange("p n t -> p (n t)"))

        def operand(quant, l):
            codes, scales = quant
            cols = slice(l * P, (l + 1) * P)
            return codes[:, cols].bitcast(FP8X4), scales[:, cols]

        def kv_matmuls(n, l):
            codes, scales = operand(xq[n], l)
            kvp[n, l] = psum.tile([P, 4, P], F32, name="kvp", tag="kvp", bufs=2)
            for t in range(4):
                nc.tensor.matmul_mx(
                    kvp[n, l][:, t, :],
                    lhsT=w_kv[:, 256 * t : 256 * (t + 1)].bitcast(FP4X4),
                    lhsT_scale=s_kv[:, P * t : P * (t + 1)],
                    rhs=codes, rhs_scale=scales,
                    start=True, stop=True,
                )

        def kv_copy(eng, n, l):
            if n not in qk:
                qk[n] = work.tile([P, TOK, 4], BF16, name="qk", tag="qk0" if n == 0 else "qk",
                                  bufs=1 if n == 0 else 2, align_bytes=64)
            copy_on(
                eng,
                qk[n][:, l * P : (l + 1) * P, :].rearrange("p (c i) t -> p c t i", i=2),
                kvp[n, l][:].rearrange("p t (c i) -> p c t i", i=2),
            )

        def kr_matmuls(n, l0=0, l1=PAIR, tag="krp"):
            for l in range(l0, l1):
                codes, scales = operand(xq[n], l)
                if n % 2 == 0:
                    if l == 0:
                        krp[n] = psum.tile([P, PAIR, H * ROT], F32, name="krp", tag=tag, bufs=2 if tag == "krp" else 1)
                    passes = ((krp[n][:, l], w_r, s_r, 0, 256, True, True),)
                else:
                    krp[n, l] = psum.tile([P, 3, H * HALF], F32, name="krp", tag="krp", bufs=2)
                    passes = (
                        (krp[n, l][:, 0:2].rearrange("p c m -> p (c m)"), w_r3, s_r3, 0, 256, True, True),
                        (krp[n, l][:, 2], w_r3, s_r3, 0, 128, True, False),
                        (krp[n, l][:, 2], w_r3, s_r3, 128, 256, False, True),
                    )
                for out, w, s, lo, hi, start, stop in passes:
                    nc.tensor.matmul_mx(
                        out, lhsT=codes, lhsT_scale=scales,
                        rhs=w[:, 2 * lo : 2 * hi].bitcast(FP4X4), rhs_scale=s[:, lo:hi],
                        start=start, stop=stop,
                    )

        def rope_products(n, l0=0, l1=PAIR):
            b, r = where(n)
            if n % 2 == 0:
                if l0 == 0:
                    prod[n] = work.tile([P, PAIR, H, 2, ROT], F32, name="prod", tag="prod", bufs=8)
                shape = [P, l1 - l0, H, 2, ROT]
                nc.vector.tensor_tensor(
                    out=prod[n][:, l0:l1],
                    in0=krp[n][:, l0:l1].rearrange("p l (h d) -> p l h d", h=H).unsqueeze(3).broadcast_to(shape),
                    in1=tab4[:, r // 4, l0:l1].rearrange("p l a c j -> p l a (c j)").unsqueeze(2).broadcast_to(shape),
                    op=MULT,
                )
                return
            for l in range(l0, l1):
                if l == 0:
                    prod[n] = work.tile([P, PAIR, H, 3, HALF], F32, name="prod", tag="prod", bufs=8)
                nc.vector.tensor_tensor(
                    out=prod[n][:, l].rearrange("p h c j -> p c h j"),
                    in0=krp[n, l][:].rearrange("p c (h j) -> p c h j", h=H),
                    in1=tab3[:, r // 4, l].unsqueeze(2).broadcast_to([P, 3, H, HALF]),
                    op=MULT,
                )

        def k_tile(n):
            if n not in kt:
                if n + 2 < NP:
                    kt[n] = work.tile([P, PAIR, H, HD], F32, name="kt", tag="qx%d" % (n + 2), bufs=1, align_bytes=64)
                else:
                    kt[n] = work.tile([P, PAIR, H, HD], F32, name="kt", bufs=2)
            return kt[n]

        def rope_sums(eng, n, l0=0, l1=PAIR):
            out = k_tile(n)[:, l0:l1].rearrange("p l h (a j) -> p (l h) a j", j=HALF)[:, :, 2:4, :]
            if n % 2 == 0:
                m = prod[n][:, l0:l1].rearrange("p l h a (c j) -> p (l h) a c j", c=2)
                eng.tensor_tensor(out=out, in0=m[:, :, :, 0, :], in1=m[:, :, :, 1, :], op=ADD)
            else:
                m = prod[n][:, l0:l1].rearrange("p l h c j -> p (l h) c j")
                eng.tensor_tensor(
                    out=out, in0=m[:, :, 2:3, :].broadcast_to([P, (l1 - l0) * H, 2, HALF]), in1=m[:, :, 0:2, :], op=SUB)

        def v_matmul(n, l):
            codes, scales = operand(kq[n], l)
            vp[n, l] = psum.tile([P, 512], F32, name="vp", tag="vp", bufs=2)
            nc.tensor.matmul_mx(
                vp[n, l][:], lhsT=codes, lhsT_scale=scales,
                rhs=w_v[:].bitcast(FP4X4), rhs_scale=s_v[:], start=True, stop=True,
            )

        def kc_matmuls(n):
            kcp[n] = psum.tile([P, PAIR, H * ROT], F32, name="kcp", tag="kcp", bufs=1)
            for l in range(PAIR):
                codes, scales = operand(kq[n], l)
                nc.tensor.matmul_mx(
                    kcp[n][:, l], lhsT=codes, lhsT_scale=scales,
                    rhs=w_k[:].bitcast(FP4X4), rhs_scale=s_k[:], start=True, stop=True,
                )

        def v_copy(eng, n, l):
            if l == 0:
                vt[n] = work.tile([P, PAIR, H * HD], F32, name="vt", bufs=4)
            copy_on(eng, vt[n][:, l, :], vp[n, l][:])

        def kc_copy(eng, n):
            copy_on(
                eng,
                k_tile(n)[:].rearrange("p l h d -> p (l h) d")[:, :, 0:ROT],
                kcp[n][:].rearrange("p l (h d) -> p (l h) d", h=H),
            )

        def store(out, tile, n, l0, l1):
            b, r = where(n)
            rows = out[b].rearrange("(p r) h d -> p r (h d)", p=P)
            nc.sync.dma_start(out=rows[:, r + l0 : r + l1, :], in_=tile[:, l0:l1])

        def store_v(n, l0=0, l1=PAIR):
            store(v_out, vt[n], n, l0, l1)

        def store_k(n, l0=0, l1=PAIR):
            store(k_out, kt[n][:].rearrange("p l h d -> p l (h d)"), n, l0, l1)

        def permute_kv_words():
            nc.scalar.copy(
                out=w_kv[:].bitcast(U16).rearrange("p (t m) -> p t m", t=4),
                in_=w_kv_raw[:].bitcast(U16).rearrange("p (m t) -> p t m", t=4))

        def permute_kv_scales():
            nc.vector.tensor_copy(
                out=s_kv[:].rearrange("p (t m) -> p t m", t=4),
                in_=s_kv_raw[:].rearrange("p (m t) -> p t m", t=4))

        rows = embt[:].rearrange("p (g o l) w j -> p g o l w j", o=2, l=PAIR)

        def table4(a):
            even = rows[:, :, 0]
            if a == 1:
                nc.vector.tensor_copy(out=tab4[:, :, :, 1], in_=even)
            else:
                nc.vector.tensor_copy(out=tab4[:, :, :, 0, 0], in_=even[:, :, :, 1])
                nc.vector.tensor_scalar(out=tab4[:, :, :, 0, 1], in0=even[:, :, :, 0], scalar1=-1.0, scalar2=None, op0=MULT)

        def table3():
            sin, cos = rows[:, :, 1, :, 0], rows[:, :, 1, :, 1]
            nc.vector.tensor_tensor(out=tab3[:, :, :, 0], in0=cos, in1=sin, op=ADD)
            nc.vector.tensor_tensor(out=tab3[:, :, :, 1], in0=cos, in1=sin, op=SUB)

        def permute_r():
            for dst, src in ((w_r3, w_r), (s_r3, s_r)):
                for a in range(2):
                    nc.scalar.copy(
                        out=dst[:].bitcast(U32).rearrange("p (a h c) -> p a h c", a=2, h=H)[:, 1 - a],
                        in_=src[:].bitcast(U32).rearrange("p (h a c) -> p a h c", a=2, h=H)[:, a])

        for n in range(LATE, NP):
            for l in range(PAIR):
                c = ((n - LATE) * PAIR + l) * HID
                xw[n, l] = late_wide[:, c : c + HID]

        def widen_late(m):
            c0 = (m - 2) // 2 * (LONG + SHORT) + m % 2 * SHORT
            c1 = min(c0 + (LONG if m % 2 else SHORT), (NP - LATE) * PAIR * HID)
            nc.gpsimd.tensor_copy(out=late_wide[:, c0:c1], in_=late_bytes[:, c0:c1].bitcast(FP8))

        V, A, G = nc.vector, nc.scalar, nc.gpsimd

        widen(V, 0, 0, 1)
        widen(V, 0, 1, 2)
        transposes(0, 0, 1, "kcp")
        transposes(0, 1, 2, "xT")
        widen(V, 1, 0, 2)
        permute_kv_words()
        transposes(1, 0, 2, "vp")
        widen(A, 2, 0, 2)
        widen(G, 3, 0, 1)
        widen(A, 3, 1, 2)
        xscale(0, 0, 1)
        xscale(0, 1, 2)
        transposes(2, 0, 2, "vp")
        widen(A, 4, 0, 2)
        permute_kv_scales()
        quantise(qx, xq, 0, "x")
        widen(G, 7, 0, 1, "qx0")
        widen(A, 5, 0, 2)
        widen(A, 6, 0, 2)
        xscale(1, 0, 2)
        kv_matmuls(0, 0)
        kv_matmuls(0, 1)
        kr_matmuls(0)
        table4(0)
        table4(1)
        quantise(qx, xq, 1, "x")
        widen(G, 8, 1, 2, "qx1")
        widen(A, 7, 1, 2)
        kv_copy(A, 0, 0)
        kv_copy(A, 0, 1)
        permute_r()
        nc.scalar.copy(out=tab3[:, :, :, 2], in_=rows[:, :, 1, :, 1])
        kv_matmuls(1, 0)
        kv_matmuls(1, 1)
        transposes(3, 0, 2, "xT")
        kv_copy(A, 1, 0)
        kv_copy(A, 1, 1)
        widen(A, 9, 0, 2)

        def outputs(n):
            v_matmul(n, 0)
            v_matmul(n, 1)
            kc_matmuls(n)

        for m in range(2, NP):
            xscale(m, 0, 2)
            if m == 2:
                quantise(qk, kq, 0, "kv")
                widen(G, 8, 0, 1, "qk0")
                outputs(0)
                kr_matmuls(1, 0, 1)
                v_copy(A, 0, 0)
                store_v(0, 0, 1)
                v_copy(A, 0, 1)
                store_v(0, 1, 2)
            rope_products(m - 2)
            quantise(qx, xq, m, "x")
            quantise(qk, kq, m - 1, "kv")
            if m == 2:
                table3()
            rope_sums(G, m - 2)
            if m < NP - 3:
                widen_late(m)
            kc_copy(A, m - 2)
            store_k(m - 2)
            if m < NP - 1:
                kr_matmuls(m - 1, (m - 1) % 2, PAIR)
            kv_matmuls(m, 0)
            if m == NP - 1:
                break
            kv_matmuls(m, 1)
            kv_copy(A, m, 0)
            kv_copy(A, m, 1)
            outputs(m - 1)
            if m + 2 < NP:
                transposes(m + 2, 0, 2, "xT")
            if m % 2:
                kr_matmuls(m, 0, 1)
            if m == NP - 2:
                kr_matmuls(m, 0, 2, "xT")
            v_copy(A, m - 1, 0)
            v_copy(A, m - 1, 1)
            store_v(m - 1)
        a, b = NP - 2, NP - 1
        v_matmul(a, 0)
        kv_matmuls(b, 1)
        v_matmul(a, 1)
        kc_matmuls(a)
        kr_matmuls(b)
        rope_products(a, 0, 1)
        rope_sums(G, a, 0, 1)
        kv_copy(V, b, 0)
        v_copy(A, a, 0)
        kv_copy(V, b, 1)
        v_copy(A, a, 1)
        store_v(a)
        rope_products(a, 1, 2)
        quantise(qk, kq, b, "kv")
        rope_sums(G, a, 1, 2)
        kc_copy(A, a)
        store_k(a)
        rope_products(b)
        rope_sums(G, b)
        outputs(b)
        v_copy(A, b, 0)
        v_copy(V, b, 1)
        store_v(b)
        kc_copy(A, b)
        store_k(b)
